import numpy as np
import ml_dtypes


def mxq(x, axis, fmt="e4m3"):
    dtype, down = {"e4m3": (ml_dtypes.float8_e4m3fn, 7), "e5m2": (ml_dtypes.float8_e5m2, 14)}[fmt]
    v = np.moveaxis(np.asarray(x, np.float32).astype(ml_dtypes.bfloat16).astype(np.float64), axis, -1)
    blocks = v.reshape(v.shape[:-1] + (-1, 32))
    amax = np.abs(blocks).max(-1, keepdims=True)
    byte = np.maximum(np.where(amax > 0, np.frexp(amax)[1] - 1 + 127, 0) - down, 1)
    scale = np.exp2(byte - 127.0)
    codes = (blocks / scale).astype(np.float32).astype(dtype).astype(np.float64)
    return np.moveaxis((codes * scale).reshape(v.shape), -1, axis)


WIDE = False


def mx_kscale(k):
    if not WIDE:
        return np.ones(k)
    levels = np.array([20, -20, 10, -10, 0])
    a = np.random.permutation(np.resize(levels, k // 512 * 4)).reshape(k // 512, 4)
    idx = np.arange(k)
    return np.exp2(a[idx // 512, idx % 128 // 32])


BF16 = ml_dtypes.bfloat16


def bf(x):
    return np.asarray(x, np.float32).astype(BF16)


def f64(x):
    return np.asarray(x).astype(np.float64)


B, NH, NW, C, K, P = 8, 8, 8, 128, 128, 4
T = P * P
N = B * NH * NW
HAD = np.array([[1.0, 1.0, 1.0, 1.0],
                [1.0, -1.0, 1.0, -1.0],
                [1.0, 1.0, -1.0, -1.0],
                [1.0, -1.0, -1.0, 1.0]])


def setup_inputs():
    s = mx_kscale(N).reshape(B, NH, NW)
    trans = np.random.standard_normal((T, B, NH, NW, C)) * s[None, :, :, :, None]
    weight = np.random.standard_normal((T, C, K)) * 0.5 * P / np.sqrt(C)
    bias = np.random.standard_normal((1, 1, 1, K)) * 0.2
    g = np.random.standard_normal((B, P * NH, P * NW, K))
    e = np.exp2(np.random.randint(-12, 1, (B, NH, NW))) / s
    e = np.repeat(np.repeat(e, P, axis=1), P, axis=2)[:, :, :, None]
    return {"trans": bf(trans), "weight": bf(weight), "bias": bf(bias), "grad_out": bf(g * e)}


def reference(trans, weight, bias, grad_out):
    x = f64(trans).reshape(T, N, C)
    g = f64(grad_out).reshape(B, NH, P, NW, P, K).transpose(2, 4, 0, 1, 3, 5)
    r = np.stack([sum(HAD[p, u] * g[p] for p in range(P)) for u in range(P)])
    gy = np.stack([sum(HAD[q, v] * r[:, q] for q in range(P)) for v in range(P)], axis=1) / T
    gy = gy.reshape(T, N, K)
    return mxq(x, 1, "e4m3").transpose(0, 2, 1) @ mxq(gy, 1, "e5m2")

@@ -1,0 +1,163 @@
+from contextlib import ExitStack
+
+import concourse.mybir as mybir
+
+FLOPS = 2 * 16 * 512 * 128 * 128
+BYTES = 2 * (16 * 512 * 128) + 2 * (8 * 32 * 32 * 128) + 4 * (16 * 128 * 128)
+
+BF16 = mybir.dt.bfloat16
+F32 = mybir.dt.float32
+U32 = mybir.dt.uint32
+U8 = mybir.dt.uint8
+E4M3_X4 = mybir.dt.float8_e4m3fn_x4
+E5M2_X4 = mybir.dt.float8_e5m2_x4
+ADD = mybir.AluOpType.add
+SUB = mybir.AluOpType.subtract
+COPY = mybir.ActivationFunctionType.Copy
+
+PARTS = 128
+PACK = 4
+SIDE = 4
+C = 128
+K = 128
+RUN = 4
+
+
+def tile_iwht3layer_pa_s_kernel(tc, trans, weight, bias, grad_out, out):
+    nc = tc.nc
+
+    g_view = grad_out.rearrange(
+        "b (i p) (h w q) k -> h w (b i) p (q k)", p=SIDE, h=2, w=PACK, q=SIDE
+    )
+    x_view = trans.rearrange("t b i (h w) c -> (b i h) t (w c)", w=PACK)
+    out_view = out.rearrange("t c k -> c t k")
+
+    with ExitStack() as ctx:
+        ctx.enter_context(tc.manual_schedule())
+        keep = ctx.enter_context(tc.tile_pool(name="keep", bufs=1))
+        work = ctx.enter_context(tc.tile_pool(name="work", bufs=2))
+        psum = ctx.enter_context(tc.psum_pool(name="psum", bufs=4))
+
+        g_raw = []
+        for w in range(PACK):
+            g_w = keep.tile([PARTS, SIDE, SIDE * K], BF16, name="g_raw%d" % w)
+            for h in range(2):
+                nc.sync.dma_start(out=g_w[h:PARTS:2], in_=g_view[h, w])
+            g_raw.append(g_w)
+        x_raw = []
+        for u in range(SIDE):
+            x_u = keep.tile([PARTS, SIDE, PACK * C], BF16, name="x_raw%d" % u)
+            nc.sync.dma_start(out=x_u[:], in_=x_view[:, SIDE * u : SIDE * (u + 1), :])
+            x_raw.append(x_u)
+
+        half_p = {}
+        done_p = keep.tile([PARTS, 2, 2, PACK, SIDE * K], F32, name="done_p")
+
+        def butterfly_p1(w):
+            half_p[w] = work.tile([PARTS, 2, 2, SIDE * K], F32, name="half_p", tag="half_p")
+            lo = g_raw[w][:, 0:2, :]
+            hi = g_raw[w][:, 2:4, :]
+            nc.vector.tensor_tensor(out=half_p[w][:, 0], in0=lo, in1=hi, op=ADD)
+            nc.vector.tensor_tensor(out=half_p[w][:, 1], in0=lo, in1=hi, op=SUB)
+
+        def butterfly_p0(w):
+            lo = half_p[w][:, :, 0]
+            hi = half_p[w][:, :, 1]
+            nc.vector.tensor_tensor(out=done_p[:, :, 0, w], in0=lo, in1=hi, op=ADD)
+            nc.vector.tensor_tensor(out=done_p[:, :, 1, w], in0=lo, in1=hi, op=SUB)
+
+        for w in range(PACK + 1):
+            if w < PACK:
+                butterfly_p1(w)
+            if w >= 1:
+                butterfly_p0(w - 1)
+
+        x_grouped = []
+        for u in range(SIDE):
+            x_g = keep.tile([PARTS, SIDE, C, PACK], BF16, name="x_grouped%d" % u, align_bytes=64)
+            for v in range(SIDE):
+                nc.scalar.copy(
+                    out=x_g[:, v].rearrange("p (r e) w -> p r w e", e=RUN),
+                    in_=x_raw[u][:, v].rearrange("p (w r e) -> p r w e", w=PACK, e=RUN),
+                )
+            x_grouped.append(x_g)
+
+        x_codes = {}
+        x_scales = {}
+
+        def quantise_x(u):
+            x_codes[u] = keep.tile([PARTS, SIDE, C], U32, name="x_codes%d" % u, align_bytes=64)
+            x_scales[u] = keep.tile([PARTS, SIDE, C], U8, name="x_scales%d" % u, align_bytes=64)
+            nc.vector.quantize_mx(
+                out=x_codes[u][:].rearrange("p v c -> p (v c)").bitcast(E4M3_X4),
+                scales=x_scales[u][:].rearrange("p v c -> p (v c)"),
+                in_=x_grouped[u][:].rearrange("p v c w -> p (v c w)"),
+            )
+
+        half_q = {}
+        gy_grouped = {}
+        gy_codes = {}
+        gy_scales = {}
+
+        def butterfly_q1(u):
+            half_q[u] = work.tile([PARTS, PACK, 2, 2, K], F32, name="half_q", tag="half_q")
+            src = done_p[:, u // 2, u % 2].rearrange("p w (a b k) -> p w a b k", a=2, b=2)
+            lo = src[:, :, 0]
+            hi = src[:, :, 1]
+            nc.vector.tensor_tensor(out=half_q[u][:, :, :, 0], in0=lo, in1=hi, op=ADD)
+            nc.vector.tensor_tensor(out=half_q[u][:, :, :, 1], in0=lo, in1=hi, op=SUB)
+
+        def butterfly_q0(u):
+            gy_grouped[u] = work.tile(
+                [PARTS, 2, 2, K, PACK], BF16, name="gy_grouped", tag="gy_grouped", align_bytes=64
+            )
+            lo = half_q[u][:, :, 0].rearrange("p w a (r e) -> p (a r) w e", e=RUN)
+            hi = half_q[u][:, :, 1].rearrange("p w a (r e) -> p (a r) w e", e=RUN)
+            for v0, op in ((0, ADD), (1, SUB)):
+                nc.vector.tensor_tensor(
+                    out=gy_grouped[u][:, v0].rearrange("p a (r e) w -> p (a r) w e", e=RUN),
+                    in0=lo,
+                    in1=hi,
+                    op=op,
+                )
+
+        def quantise_gy(u):
+            gy_codes[u] = keep.tile([PARTS, SIDE * K], U32, name="gy_codes%d" % u, align_bytes=64)
+            gy_scales[u] = keep.tile([PARTS, SIDE * K], U8, name="gy_scales%d" % u, align_bytes=64)
+            nc.vector.quantize_mx(
+                out=gy_codes[u][:].bitcast(E5M2_X4),
+                scales=gy_scales[u][:],
+                in_=gy_grouped[u][:].rearrange("p b a k w -> p (b a k w)"),
+            )
+
+        def multiply_and_store(u):
+            result = work.tile([PARTS, SIDE, K], F32, name="result", tag="result")
+            for v in range(SIDE):
+                place = 2 * (v % 2) + v // 2
+                acc = psum.tile([PARTS, SIDE * K], F32, name="acc", tag="acc")
+                nc.tensor.matmul_mx(
+                    out=acc[:],
+                    lhsT=x_codes[u][:, v, :].bitcast(E4M3_X4),
+                    lhsT_scale=x_scales[u][:, v, :],
+                    rhs=gy_codes[u][:].bitcast(E5M2_X4),
+                    rhs_scale=gy_scales[u][:],
+                    start=True,
+                    stop=True,
+                )
+                nc.scalar.activation(
+                    out=result[:, v, :],
+                    in_=acc[:, K * place : K * (place + 1)],
+                    func=COPY,
+                    scale=1.0 / (SIDE * SIDE),
+                )
+            nc.sync.dma_start(out=out_view[:, SIDE * u : SIDE * (u + 1), :], in_=result[:])
+
+        for u in range(SIDE + 2):
+            if u < SIDE:
+                butterfly_q1(u)
+                quantise_x(u)
+            if 1 <= u <= SIDE:
+                butterfly_q0(u - 1)
+            if u >= 2:
+                quantise_gy(u - 2)
+                multiply_and_store(u - 2)

@@ -9,6 +9,7 @@ BF16 = mybir.dt.bfloat16
 F32 = mybir.dt.float32
 U32 = mybir.dt.uint32
 U8 = mybir.dt.uint8
+I32 = mybir.dt.int32
 E4M3_X4 = mybir.dt.float8_e4m3fn_x4
 E5M2_X4 = mybir.dt.float8_e5m2_x4
 ADD = mybir.AluOpType.add
@@ -21,6 +22,8 @@ SIDE = 4
 C = 128
 K = 128
 RUN = 4
+N_PASS = 512
+PAD_BLOCKS = N_PASS // K - 1
 
 
 def tile_iwht3layer_pa_s_kernel(tc, trans, weight, bias, grad_out, out):
@@ -30,12 +33,13 @@ def tile_iwht3layer_pa_s_kernel(tc, trans, weight, bias, grad_out, out):
         "b (i p) (h w q) k -> h w (b i) p (q k)", p=SIDE, h=2, w=PACK, q=SIDE
     )
     x_view = trans.rearrange("t b i (h w) c -> (b i h) t (w c)", w=PACK)
-    out_view = out.rearrange("t c k -> c t k")
+    out_view = out.rearrange("(u a b) c k -> c u b a k", a=2, b=2)
 
     with ExitStack() as ctx:
         ctx.enter_context(tc.manual_schedule())
         keep = ctx.enter_context(tc.tile_pool(name="keep", bufs=1))
         work = ctx.enter_context(tc.tile_pool(name="work", bufs=2))
+        outs = ctx.enter_context(tc.tile_pool(name="outs", bufs=4))
         psum = ctx.enter_context(tc.psum_pool(name="psum", bufs=4))
 
         g_raw = []
@@ -49,6 +53,12 @@ def tile_iwht3layer_pa_s_kernel(tc, trans, weight, bias, grad_out, out):
             x_u = keep.tile([PARTS, SIDE, PACK * C], BF16, name="x_raw%d" % u)
             nc.sync.dma_start(out=x_u[:], in_=x_view[:, SIDE * u : SIDE * (u + 1), :])
             x_raw.append(x_u)
+
+        gy_width = (PAD_BLOCKS + SIDE * SIDE) * K
+        gy_codes = keep.tile([PARTS, gy_width], U32, name="gy_codes", align_bytes=64)
+        gy_scales = keep.tile([PARTS, gy_width], U8, name="gy_scales", align_bytes=64)
+        nc.vector.memset(gy_codes[:, 0 : PAD_BLOCKS * K].bitcast(I32), 0)
+        nc.vector.memset(gy_scales[:, 0 : PAD_BLOCKS * K].bitcast(I32), 0)
 
         half_p = {}
         done_p = keep.tile([PARTS, 2, 2, PACK, SIDE * K], F32, name="done_p")
@@ -95,9 +105,6 @@ def tile_iwht3layer_pa_s_kernel(tc, trans, weight, bias, grad_out, out):
             )
 
         half_q = {}
-        gy_grouped = {}
-        gy_codes = {}
-        gy_scales = {}
 
         def butterfly_q1(u):
             half_q[u] = work.tile([PARTS, PACK, 2, 2, K], F32, name="half_q", tag="half_q")
@@ -107,57 +114,57 @@ def tile_iwht3layer_pa_s_kernel(tc, trans, weight, bias, grad_out, out):
             nc.vector.tensor_tensor(out=half_q[u][:, :, :, 0], in0=lo, in1=hi, op=ADD)
             nc.vector.tensor_tensor(out=half_q[u][:, :, :, 1], in0=lo, in1=hi, op=SUB)
 
-        def butterfly_q0(u):
-            gy_grouped[u] = work.tile(
-                [PARTS, 2, 2, K, PACK], BF16, name="gy_grouped", tag="gy_grouped", align_bytes=64
-            )
-            lo = half_q[u][:, :, 0].rearrange("p w a (r e) -> p (a r) w e", e=RUN)
-            hi = half_q[u][:, :, 1].rearrange("p w a (r e) -> p (a r) w e", e=RUN)
-            for v0, op in ((0, ADD), (1, SUB)):
-                nc.vector.tensor_tensor(
-                    out=gy_grouped[u][:, v0].rearrange("p a (r e) w -> p (a r) w e", e=RUN),
-                    in0=lo,
-                    in1=hi,
-                    op=op,
-                )
+        pairs = [(u, v0) for u in range(SIDE) for v0 in range(2)]
+        gy_grouped = {}
 
-        def quantise_gy(u):
-            gy_codes[u] = keep.tile([PARTS, SIDE * K], U32, name="gy_codes%d" % u, align_bytes=64)
-            gy_scales[u] = keep.tile([PARTS, SIDE * K], U8, name="gy_scales%d" % u, align_bytes=64)
+        def butterfly_q0(u, v0):
+            gy_grouped[u, v0] = work.tile(
+                [PARTS, 2, K, PACK], BF16, name="gy_grouped", tag="gy_grouped", align_bytes=64
+            )
+            nc.vector.tensor_tensor(
+                out=gy_grouped[u, v0][:].rearrange("p a (r e) w -> p (a r) w e", e=RUN),
+                in0=half_q[u][:, :, 0].rearrange("p w a (r e) -> p (a r) w e", e=RUN),
+                in1=half_q[u][:, :, 1].rearrange("p w a (r e) -> p (a r) w e", e=RUN),
+                op=(ADD, SUB)[v0],
+            )
+
+
+        def finish(u, v0):
+            first = 2 * pairs.index((u, v0))
+            fresh = slice((PAD_BLOCKS + first) * K, (PAD_BLOCKS + first + 2) * K)
             nc.vector.quantize_mx(
-                out=gy_codes[u][:].bitcast(E5M2_X4),
-                scales=gy_scales[u][:],
-                in_=gy_grouped[u][:].rearrange("p b a k w -> p (b a k w)"),
+                out=gy_codes[:, fresh].bitcast(E5M2_X4),
+                scales=gy_scales[:, fresh],
+                in_=gy_grouped[u, v0][:].rearrange("p a k w -> p (a k w)"),
             )
-
-        def multiply_and_store(u):
-            result = work.tile([PARTS, SIDE, K], F32, name="result", tag="result")
-            for v in range(SIDE):
-                place = 2 * (v % 2) + v // 2
-                acc = psum.tile([PARTS, SIDE * K], F32, name="acc", tag="acc")
+            result = outs.tile([PARTS, 2, K], F32, name="result", tag="result")
+            for v1 in range(2):
+                window = slice((first + v1) * K, (first + v1) * K + N_PASS)
+                acc = psum.tile([PARTS, N_PASS], F32, name="acc", tag="acc")
                 nc.tensor.matmul_mx(
                     out=acc[:],
-                    lhsT=x_codes[u][:, v, :].bitcast(E4M3_X4),
-                    lhsT_scale=x_scales[u][:, v, :],
-                    rhs=gy_codes[u][:].bitcast(E5M2_X4),
-                    rhs_scale=gy_scales[u][:],
+                    lhsT=x_codes[u][:, 2 * v1 + v0, :].bitcast(E4M3_X4),
+                    lhsT_scale=x_scales[u][:, 2 * v1 + v0, :],
+                    rhs=gy_codes[:, window].bitcast(E5M2_X4),
+                    rhs_scale=gy_scales[:, window],
                     start=True,
                     stop=True,
                 )
                 nc.scalar.activation(
-                    out=result[:, v, :],
-                    in_=acc[:, K * place : K * (place + 1)],
+                    out=result[:, v1, :],
+                    in_=acc[:, N_PASS - K : N_PASS],
                     func=COPY,
                     scale=1.0 / (SIDE * SIDE),
                 )
-            nc.sync.dma_start(out=out_view[:, SIDE * u : SIDE * (u + 1), :], in_=result[:])
+            nc.sync.dma_start(out=out_view[:, u, v0], in_=result[:])
 
-        for u in range(SIDE + 2):
-            if u < SIDE:
-                butterfly_q1(u)
-                quantise_x(u)
-            if 1 <= u <= SIDE:
-                butterfly_q0(u - 1)
-            if u >= 2:
-                quantise_gy(u - 2)
-                multiply_and_store(u - 2)
+        butterfly_q1(0)
+        quantise_x(0)
+        for i, (u, v0) in enumerate(pairs):
+            if v0 == 0 and u + 1 < SIDE:
+                butterfly_q1(u + 1)
+                quantise_x(u + 1)
+            butterfly_q0(u, v0)
+            if i >= 1:
+                finish(*pairs[i - 1])
+        finish(*pairs[-1])

@@ -38,7 +38,7 @@ def tile_iwht3layer_pa_s_kernel(tc, trans, weight, bias, grad_out, out):
     with ExitStack() as ctx:
         ctx.enter_context(tc.manual_schedule())
         keep = ctx.enter_context(tc.tile_pool(name="keep", bufs=1))
-        work = ctx.enter_context(tc.tile_pool(name="work", bufs=2))
+        work = ctx.enter_context(tc.tile_pool(name="work", bufs=4))
         outs = ctx.enter_context(tc.tile_pool(name="outs", bufs=4))
         psum = ctx.enter_context(tc.psum_pool(name="psum", bufs=4))
 
@@ -60,28 +60,6 @@ def tile_iwht3layer_pa_s_kernel(tc, trans, weight, bias, grad_out, out):
         nc.vector.memset(gy_codes[:, 0 : PAD_BLOCKS * K].bitcast(I32), 0)
         nc.vector.memset(gy_scales[:, 0 : PAD_BLOCKS * K].bitcast(I32), 0)
 
-        half_p = {}
-        done_p = keep.tile([PARTS, 2, 2, PACK, SIDE * K], F32, name="done_p")
-
-        def butterfly_p1(w):
-            half_p[w] = work.tile([PARTS, 2, 2, SIDE * K], F32, name="half_p", tag="half_p")
-            lo = g_raw[w][:, 0:2, :]
-            hi = g_raw[w][:, 2:4, :]
-            nc.vector.tensor_tensor(out=half_p[w][:, 0], in0=lo, in1=hi, op=ADD)
-            nc.vector.tensor_tensor(out=half_p[w][:, 1], in0=lo, in1=hi, op=SUB)
-
-        def butterfly_p0(w):
-            lo = half_p[w][:, :, 0]
-            hi = half_p[w][:, :, 1]
-            nc.vector.tensor_tensor(out=done_p[:, :, 0, w], in0=lo, in1=hi, op=ADD)
-            nc.vector.tensor_tensor(out=done_p[:, :, 1, w], in0=lo, in1=hi, op=SUB)
-
-        for w in range(PACK + 1):
-            if w < PACK:
-                butterfly_p1(w)
-            if w >= 1:
-                butterfly_p0(w - 1)
-
         x_grouped = []
         for u in range(SIDE):
             x_g = keep.tile([PARTS, SIDE, C, PACK], BF16, name="x_grouped%d" % u, align_bytes=64)
@@ -92,27 +70,44 @@ def tile_iwht3layer_pa_s_kernel(tc, trans, weight, bias, grad_out, out):
                 )
             x_grouped.append(x_g)
 
-        x_codes = {}
-        x_scales = {}
+        half_p = [keep.tile([PARTS, PACK, 2, SIDE * K], F32, name="half_p%d" % a) for a in range(2)]
+        done_p = [keep.tile([PARTS, 2, PACK, SIDE * K], F32, name="done_p%d" % a) for a in range(2)]
+        half_q = [keep.tile([PARTS, 2, PACK, 2, 2, K], F32, name="half_q%d" % a) for a in range(2)]
+        both = ((0, ADD), (1, SUB))
 
-        def quantise_x(u):
-            x_codes[u] = keep.tile([PARTS, SIDE, C], U32, name="x_codes%d" % u, align_bytes=64)
-            x_scales[u] = keep.tile([PARTS, SIDE, C], U8, name="x_scales%d" % u, align_bytes=64)
+        for w in range(PACK):
+            for u1, op in both:
+                nc.vector.tensor_tensor(
+                    out=half_p[u1][:, w], in0=g_raw[w][:, 0:2, :], in1=g_raw[w][:, 2:4, :], op=op
+                )
+        for u1 in range(2):
+            for u0, op in both:
+                nc.vector.tensor_tensor(
+                    out=done_p[u1][:, u0], in0=half_p[u1][:, :, 0], in1=half_p[u1][:, :, 1], op=op
+                )
+        for u1 in range(2):
+            src = done_p[u1][:].rearrange("p b w (a r) -> p (b w) a r", a=2)
+            dst = half_q[u1][:].rearrange("p b w c a k -> p (b w) c a k")
+            for v1, op in both:
+                nc.vector.tensor_tensor(
+                    out=dst[:, :, :, v1],
+                    in0=src[:, :, 0].rearrange("p m (c k) -> p m c k", c=2),
+                    in1=src[:, :, 1].rearrange("p m (c k) -> p m c k", c=2),
+                    op=op,
+                )
+
+        x_codes = []
+        x_scales = []
+        for u in range(SIDE):
+            codes = keep.tile([PARTS, SIDE, C], U32, name="x_codes%d" % u, align_bytes=64)
+            scales = keep.tile([PARTS, SIDE, C], U8, name="x_scales%d" % u, align_bytes=64)
             nc.vector.quantize_mx(
-                out=x_codes[u][:].rearrange("p v c -> p (v c)").bitcast(E4M3_X4),
-                scales=x_scales[u][:].rearrange("p v c -> p (v c)"),
+                out=codes[:].rearrange("p v c -> p (v c)").bitcast(E4M3_X4),
+                scales=scales[:].rearrange("p v c -> p (v c)"),
                 in_=x_grouped[u][:].rearrange("p v c w -> p (v c w)"),
             )
-
-        half_q = {}
-
-        def butterfly_q1(u):
-            half_q[u] = work.tile([PARTS, PACK, 2, 2, K], F32, name="half_q", tag="half_q")
-            src = done_p[:, u // 2, u % 2].rearrange("p w (a b k) -> p w a b k", a=2, b=2)
-            lo = src[:, :, 0]
-            hi = src[:, :, 1]
-            nc.vector.tensor_tensor(out=half_q[u][:, :, :, 0], in0=lo, in1=hi, op=ADD)
-            nc.vector.tensor_tensor(out=half_q[u][:, :, :, 1], in0=lo, in1=hi, op=SUB)
+            x_codes.append(codes)
+            x_scales.append(scales)
 
         pairs = [(u, v0) for u in range(SIDE) for v0 in range(2)]
         gy_grouped = {}
@@ -121,13 +116,13 @@ def tile_iwht3layer_pa_s_kernel(tc, trans, weight, bias, grad_out, out):
             gy_grouped[u, v0] = work.tile(
                 [PARTS, 2, K, PACK], BF16, name="gy_grouped", tag="gy_grouped", align_bytes=64
             )
+            src = half_q[u // 2][:, u % 2]
             nc.vector.tensor_tensor(
                 out=gy_grouped[u, v0][:].rearrange("p a (r e) w -> p (a r) w e", e=RUN),
-                in0=half_q[u][:, :, 0].rearrange("p w a (r e) -> p (a r) w e", e=RUN),
-                in1=half_q[u][:, :, 1].rearrange("p w a (r e) -> p (a r) w e", e=RUN),
-                op=(ADD, SUB)[v0],
+                in0=src[:, :, 0].rearrange("p w a (r e) -> p (a r) w e", e=RUN),
+                in1=src[:, :, 1].rearrange("p w a (r e) -> p (a r) w e", e=RUN),
+                op=both[v0][1],
             )
-
 
         def finish(u, v0):
             first = 2 * pairs.index((u, v0))
@@ -158,13 +153,8 @@ def tile_iwht3layer_pa_s_kernel(tc, trans, weight, bias, grad_out, out):
                 )
             nc.sync.dma_start(out=out_view[:, u, v0], in_=result[:])
 
-        butterfly_q1(0)
-        quantise_x(0)
-        for i, (u, v0) in enumerate(pairs):
-            if v0 == 0 and u + 1 < SIDE:
-                butterfly_q1(u + 1)
-                quantise_x(u + 1)
-            butterfly_q0(u, v0)
-            if i >= 1:
-                finish(*pairs[i - 1])
-        finish(*pairs[-1])
+        for u in range(SIDE):
+            for v0 in range(2):
+                butterfly_q0(u, v0)
+            for v0 in range(2):
+                finish(u, v0)

@@ -1,6 +1,7 @@
 from contextlib import ExitStack
 
 import concourse.mybir as mybir
+from concourse.masks import make_identity
 
 FLOPS = 2 * 16 * 512 * 128 * 128
 BYTES = 2 * (16 * 512 * 128) + 2 * (8 * 32 * 32 * 128) + 4 * (16 * 128 * 128)
@@ -24,30 +25,39 @@ K = 128
 RUN = 4
 N_PASS = 512
 PAD_BLOCKS = N_PASS // K - 1
+SLOT = PARTS // PACK
+SLOTS = 2
+K_PE = SLOT * SLOTS
+K_VE = K - K_PE
+PLUS = ((0, 1, 2, 3), (0, 2), (0, 1), (0, 3))
+BLOCK_OF_U = (0, 2, 1, 3)
 
 
 def tile_iwht3layer_pa_s_kernel(tc, trans, weight, bias, grad_out, out):
     nc = tc.nc
 
     g_view = grad_out.rearrange(
-        "b (i p) (h w q) k -> h w (b i) p (q k)", p=SIDE, h=2, w=PACK, q=SIDE
+        "b (i p) (h w q) k -> h p (b i) (w q k)", p=SIDE, h=2, w=PACK, q=SIDE
     )
     x_view = trans.rearrange("t b i (h w) c -> (b i h) t (w c)", w=PACK)
-    out_view = out.rearrange("(u a b) c k -> c u b a k", a=2, b=2)
+    out_view = out.rearrange("(a b v) c k -> c v b a k", a=2, b=2)
 
     with ExitStack() as ctx:
         ctx.enter_context(tc.manual_schedule())
         keep = ctx.enter_context(tc.tile_pool(name="keep", bufs=1))
-        work = ctx.enter_context(tc.tile_pool(name="work", bufs=4))
         outs = ctx.enter_context(tc.tile_pool(name="outs", bufs=4))
-        psum = ctx.enter_context(tc.psum_pool(name="psum", bufs=4))
+        flip = ctx.enter_context(tc.psum_pool(name="flip", bufs=6))
+        accs = ctx.enter_context(tc.psum_pool(name="accs", bufs=2))
+
+        ident = keep.tile([PARTS, PARTS], F32, name="ident")
+        make_identity(nc, ident[:])
 
         g_raw = []
-        for w in range(PACK):
-            g_w = keep.tile([PARTS, SIDE, SIDE * K], BF16, name="g_raw%d" % w)
+        for p in range(SIDE):
+            g_p = keep.tile([PARTS, PACK * SIDE * K], BF16, name="g_raw%d" % p)
             for h in range(2):
-                nc.sync.dma_start(out=g_w[h:PARTS:2], in_=g_view[h, w])
-            g_raw.append(g_w)
+                nc.sync.dma_start(out=g_p[h:PARTS:2], in_=g_view[h, p])
+            g_raw.append(g_p[:].rearrange("p (w q k) -> p w q k", w=PACK, q=SIDE))
         x_raw = []
         for u in range(SIDE):
             x_u = keep.tile([PARTS, SIDE, PACK * C], BF16, name="x_raw%d" % u)
@@ -60,101 +70,220 @@ def tile_iwht3layer_pa_s_kernel(tc, trans, weight, bias, grad_out, out):
         nc.vector.memset(gy_codes[:, 0 : PAD_BLOCKS * K].bitcast(I32), 0)
         nc.vector.memset(gy_scales[:, 0 : PAD_BLOCKS * K].bitcast(I32), 0)
 
-        x_grouped = []
-        for u in range(SIDE):
-            x_g = keep.tile([PARTS, SIDE, C, PACK], BF16, name="x_grouped%d" % u, align_bytes=64)
-            for v in range(SIDE):
-                nc.scalar.copy(
-                    out=x_g[:, v].rearrange("p (r e) w -> p r w e", e=RUN),
-                    in_=x_raw[u][:, v].rearrange("p (w r e) -> p r w e", w=PACK, e=RUN),
-                )
-            x_grouped.append(x_g)
-
-        half_p = [keep.tile([PARTS, PACK, 2, SIDE * K], F32, name="half_p%d" % a) for a in range(2)]
-        done_p = [keep.tile([PARTS, 2, PACK, SIDE * K], F32, name="done_p%d" % a) for a in range(2)]
-        half_q = [keep.tile([PARTS, 2, PACK, 2, 2, K], F32, name="half_q%d" % a) for a in range(2)]
+        gy_grouped = keep.tile([PARTS, SIDE * SIDE, K, PACK], BF16, name="gy_grouped", align_bytes=64)
+        gy_by_place = gy_grouped[:].rearrange("p (v b) k w -> p b v k w", b=SIDE)
         both = ((0, ADD), (1, SUB))
 
-        for w in range(PACK):
-            for u1, op in both:
-                nc.vector.tensor_tensor(
-                    out=half_p[u1][:, w], in0=g_raw[w][:, 0:2, :], in1=g_raw[w][:, 2:4, :], op=op
+        g_f32 = [
+            keep.tile([PARTS, SIDE, SLOTS, PACK, SLOT], F32, name="g_f32_%d" % p) for p in range(SIDE)
+        ]
+        turned = [
+            [keep.tile([PARTS, SIDE, PARTS], F32, name="turned%d_%d" % (s, v)) for v in range(SIDE)]
+            for s in range(SLOTS)
+        ]
+
+        def cast(p, s):
+            nc.scalar.activation(
+                out=g_f32[p][:, :, s],
+                in_=g_raw[p][:, :, :, SLOT * s : SLOT * (s + 1)].rearrange("p w q e -> p q w e"),
+                func=COPY,
+                scale=4.0,
+            )
+
+        def add_up(dst, terms):
+            for i, term in enumerate(terms):
+                nc.tensor.matmul(
+                    out=dst,
+                    lhsT=term,
+                    rhs=ident[:],
+                    is_transpose=True,
+                    start=(i == 0),
+                    stop=(i == len(terms) - 1),
                 )
-        for u1 in range(2):
-            for u0, op in both:
-                nc.vector.tensor_tensor(
-                    out=done_p[u1][:, u0], in0=half_p[u1][:, :, 0], in1=half_p[u1][:, :, 1], op=op
-                )
-        for u1 in range(2):
-            src = done_p[u1][:].rearrange("p b w (a r) -> p (b w) a r", a=2)
-            dst = half_q[u1][:].rearrange("p b w c a k -> p (b w) c a k")
+
+        def new_bank(shape):
+            return flip.tile(shape, F32, name="bank", tag="bank")
+
+        def turn_q(bank, s, p, g):
+            add_up(bank[:, p, :], [g_f32[p][:, q, s].rearrange("p w e -> p (w e)") for q in PLUS[g]])
+
+        def half_out_q(bank, s):
+            nc.scalar.activation(out=turned[s][0][:], in_=bank[:], func=COPY, scale=0.5)
+
+        def rest_out_q(bank, s, v):
+            nc.vector.tensor_tensor(out=turned[s][v][:], in0=bank[:], in1=turned[s][0][:], op=SUB)
+
+        def turn_p(pair, g):
+            bank = new_bank([PARTS, 2, SLOTS, PARTS])
+            for a in range(2):
+                for s in range(SLOTS):
+                    add_up(bank[:, a, s, :], [turned[s][2 * pair + a][:, p, :] for p in PLUS[g]])
+            return bank
+
+        def half_out_p(bank, pair):
+            half_sum = keep.tile([PARTS, 2, K_PE, PACK], F32, name="half_sum%d" % pair)
+            nc.scalar.activation(
+                out=half_sum[:].rearrange("p a (s e) w -> p a s e w", s=SLOTS),
+                in_=bank[:].rearrange("p a s (w e) -> p a s e w", w=PACK),
+                func=COPY,
+                scale=0.5,
+            )
+            nc.scalar.copy(
+                out=gy_by_place[:, BLOCK_OF_U[0], 2 * pair : 2 * pair + 2, 0:K_PE, :], in_=half_sum[:]
+            )
+            return half_sum
+
+        def rest_out_p(bank, half_sum, pair, u):
+            nc.vector.tensor_tensor(
+                out=gy_by_place[:, BLOCK_OF_U[u], 2 * pair : 2 * pair + 2, 0:K_PE, :].rearrange(
+                    "p a (s e) w -> p a s e w", s=SLOTS
+                ),
+                in0=bank[:].rearrange("p a s (w e) -> p a s e w", w=PACK),
+                in1=half_sum[:].rearrange("p a (s e) w -> p a s e w", s=SLOTS),
+                op=SUB,
+            )
+
+        half_q = [keep.tile([PARTS, SIDE, PACK, 2, K_VE], F32, name="half_q%d" % a) for a in range(2)]
+        done_q = [keep.tile([PARTS, 2, SIDE, PACK, K_VE], F32, name="done_q%d" % a) for a in range(2)]
+        half_p = [keep.tile([PARTS, 2, 2, PACK, 2, K_VE], F32, name="half_p%d" % a) for a in range(2)]
+
+        def step_q1(p):
             for v1, op in both:
                 nc.vector.tensor_tensor(
-                    out=dst[:, :, :, v1],
-                    in0=src[:, :, 0].rearrange("p m (c k) -> p m c k", c=2),
-                    in1=src[:, :, 1].rearrange("p m (c k) -> p m c k", c=2),
+                    out=half_q[v1][:, p],
+                    in0=g_raw[p][:, :, 0:2, K_PE:K],
+                    in1=g_raw[p][:, :, 2:4, K_PE:K],
                     op=op,
                 )
 
-        x_codes = []
-        x_scales = []
-        for u in range(SIDE):
-            codes = keep.tile([PARTS, SIDE, C], U32, name="x_codes%d" % u, align_bytes=64)
-            scales = keep.tile([PARTS, SIDE, C], U8, name="x_scales%d" % u, align_bytes=64)
+        def step_q0(v1):
+            for v0, op in both:
+                nc.vector.tensor_tensor(
+                    out=done_q[v1][:, v0],
+                    in0=half_q[v1][:, :, :, 0, :],
+                    in1=half_q[v1][:, :, :, 1, :],
+                    op=op,
+                )
+
+        def step_p1(v1):
+            src = done_q[v1][:].rearrange("p v (a b) w k -> p a v (b w) k", a=2)
+            dst = half_p[v1][:].rearrange("p v b w a k -> p a v (b w) k")
+            for u1, op in both:
+                nc.vector.tensor_tensor(out=dst[:, u1], in0=src[:, 0], in1=src[:, 1], op=op)
+
+        def step_p0(v, u0):
+            src = half_p[v // 2][:, v % 2]
+            first = SIDE * v + 2 * u0
+            nc.vector.tensor_tensor(
+                out=gy_grouped[:, first : first + 2, K_PE:K, :],
+                in0=src[:, 0].rearrange("p w a k -> p a k w"),
+                in1=src[:, 1].rearrange("p w a k -> p a k w"),
+                op=both[u0][1],
+            )
+
+        x_grouped = [
+            keep.tile([PARTS, SIDE, C, PACK], BF16, name="x_grouped%d" % u, align_bytes=64)
+            for u in range(SIDE)
+        ]
+        x_codes = [keep.tile([PARTS, SIDE, C], U32, name="x_codes%d" % u, align_bytes=64) for u in range(SIDE)]
+        x_scales = [keep.tile([PARTS, SIDE, C], U8, name="x_scales%d" % u, align_bytes=64) for u in range(SIDE)]
+
+        def regroup(u, v):
+            nc.scalar.copy(
+                out=x_grouped[u][:, v].rearrange("p (r e) w -> p r w e", e=RUN),
+                in_=x_raw[u][:, v].rearrange("p (w r e) -> p r w e", w=PACK, e=RUN),
+            )
+
+        def quantise_x(u):
             nc.vector.quantize_mx(
-                out=codes[:].rearrange("p v c -> p (v c)").bitcast(E4M3_X4),
-                scales=scales[:].rearrange("p v c -> p (v c)"),
+                out=x_codes[u][:].rearrange("p v c -> p (v c)").bitcast(E4M3_X4),
+                scales=x_scales[u][:].rearrange("p v c -> p (v c)"),
                 in_=x_grouped[u][:].rearrange("p v c w -> p (v c w)"),
             )
-            x_codes.append(codes)
-            x_scales.append(scales)
 
-        pairs = [(u, v0) for u in range(SIDE) for v0 in range(2)]
-        gy_grouped = {}
-
-        def butterfly_q0(u, v0):
-            gy_grouped[u, v0] = work.tile(
-                [PARTS, 2, K, PACK], BF16, name="gy_grouped", tag="gy_grouped", align_bytes=64
-            )
-            src = half_q[u // 2][:, u % 2]
-            nc.vector.tensor_tensor(
-                out=gy_grouped[u, v0][:].rearrange("p a (r e) w -> p (a r) w e", e=RUN),
-                in0=src[:, :, 0].rearrange("p w a (r e) -> p (a r) w e", e=RUN),
-                in1=src[:, :, 1].rearrange("p w a (r e) -> p (a r) w e", e=RUN),
-                op=both[v0][1],
-            )
-
-        def finish(u, v0):
-            first = 2 * pairs.index((u, v0))
+        def finish(v, u0):
+            first = SIDE * v + 2 * u0
             fresh = slice((PAD_BLOCKS + first) * K, (PAD_BLOCKS + first + 2) * K)
             nc.vector.quantize_mx(
                 out=gy_codes[:, fresh].bitcast(E5M2_X4),
                 scales=gy_scales[:, fresh],
-                in_=gy_grouped[u, v0][:].rearrange("p a k w -> p (a k w)"),
+                in_=gy_grouped[:, first : first + 2].rearrange("p a k w -> p (a k w)"),
             )
             result = outs.tile([PARTS, 2, K], F32, name="result", tag="result")
-            for v1 in range(2):
-                window = slice((first + v1) * K, (first + v1) * K + N_PASS)
-                acc = psum.tile([PARTS, N_PASS], F32, name="acc", tag="acc")
+            for u1 in range(2):
+                window = slice((first + u1) * K, (first + u1) * K + N_PASS)
+                acc = accs.tile([PARTS, N_PASS], F32, name="acc", tag="acc")
                 nc.tensor.matmul_mx(
                     out=acc[:],
-                    lhsT=x_codes[u][:, 2 * v1 + v0, :].bitcast(E4M3_X4),
-                    lhsT_scale=x_scales[u][:, 2 * v1 + v0, :],
+                    lhsT=x_codes[2 * u1 + u0][:, v, :].bitcast(E4M3_X4),
+                    lhsT_scale=x_scales[2 * u1 + u0][:, v, :],
                     rhs=gy_codes[:, window].bitcast(E5M2_X4),
                     rhs_scale=gy_scales[:, window],
                     start=True,
                     stop=True,
                 )
                 nc.scalar.activation(
-                    out=result[:, v1, :],
+                    out=result[:, u1, :],
                     in_=acc[:, N_PASS - K : N_PASS],
                     func=COPY,
                     scale=1.0 / (SIDE * SIDE),
                 )
-            nc.sync.dma_start(out=out_view[:, u, v0], in_=result[:])
+            nc.sync.dma_start(out=out_view[:, v, u0], in_=result[:])
 
+        def regroup_range(start, stop):
+            for t in range(start, stop):
+                regroup(t // SIDE, t % SIDE)
+
+        first_banks = [new_bank([PARTS, SIDE, PARTS]) for g in range(SIDE)]
+        for p in range(SIDE):
+            cast(p, 0)
+            cast(p, 1)
+            step_q1(p)
+            for g in range(SIDE):
+                turn_q(first_banks[g], 0, p, g)
+        regroup_range(0, 1)
+        half_out_q(first_banks[0], 0)
+        step_q0(0)
+        step_q0(1)
+        second_banks = []
+        for g in range(2):
+            second_banks.append(new_bank([PARTS, SIDE, PARTS]))
+            for p in range(SIDE):
+                turn_q(second_banks[g], 1, p, g)
+        regroup_range(1, 5)
+        half_out_q(second_banks[0], 1)
+        for v in range(1, SIDE):
+            rest_out_q(first_banks[v], 0, v)
+        for g in range(2, SIDE):
+            second_banks.append(new_bank([PARTS, SIDE, PARTS]))
+            for p in range(SIDE):
+                turn_q(second_banks[g], 1, p, g)
+        for v in range(1, SIDE):
+            rest_out_q(second_banks[v], 1, v)
+
+        banks = [turn_p(0, g) for g in range(SIDE)]
+        regroup_range(5, SIDE * SIDE)
+        step_p1(0)
+        step_p1(1)
+        for v in range(2):
+            for u0 in range(2):
+                step_p0(v, u0)
+        half_sum = half_out_p(banks[0], 0)
+        for u in (2, 1, 3):
+            rest_out_p(banks[u], half_sum, 0, u)
+
+        banks = [turn_p(1, g) for g in range(SIDE)]
+        half_sum = half_out_p(banks[0], 1)
         for u in range(SIDE):
-            for v0 in range(2):
-                butterfly_q0(u, v0)
-            for v0 in range(2):
-                finish(u, v0)
+            quantise_x(u)
+        for v in range(2):
+            for u0 in range(2):
+                finish(v, u0)
+        for v in range(2, SIDE):
+            for u0 in range(2):
+                step_p0(v, u0)
+        for u in (2, 1, 3):
+            rest_out_p(banks[u], half_sum, 1, u)
+        for v in range(2, SIDE):
+            for u0 in range(2):
+                finish(v, u0)

@@ -39,30 +39,32 @@ def tile_iwht3layer_pa_s_kernel(tc, trans, weight, bias, grad_out, out):
     g_view = grad_out.rearrange(
         "b (i p) (h w q) k -> h p (b i) (w q k)", p=SIDE, h=2, w=PACK, q=SIDE
     )
-    x_view = trans.rearrange("t b i (h w) c -> (b i h) t (w c)", w=PACK)
+    x_view = trans.rearrange("(u v) b i (h w) c -> (b i h) v u (w c)", v=SIDE, w=PACK)
     out_view = out.rearrange("(a b v) c k -> c v b a k", a=2, b=2)
 
     with ExitStack() as ctx:
         ctx.enter_context(tc.manual_schedule())
         keep = ctx.enter_context(tc.tile_pool(name="keep", bufs=1))
         outs = ctx.enter_context(tc.tile_pool(name="outs", bufs=4))
-        flip = ctx.enter_context(tc.psum_pool(name="flip", bufs=6))
-        accs = ctx.enter_context(tc.psum_pool(name="accs", bufs=2))
+        psum = ctx.enter_context(tc.psum_pool(name="psum", bufs=8))
 
         ident = keep.tile([PARTS, PARTS], F32, name="ident")
         make_identity(nc, ident[:])
 
-        g_raw = []
+        g_tiles = [keep.tile([PARTS, 1, PACK * SIDE * K], BF16, name="g_raw%d" % p) for p in range(SIDE)]
+        g_place = ((0, 0), (1, 0), (2, 0), (3, 0))
         for p in range(SIDE):
-            g_p = keep.tile([PARTS, PACK * SIDE * K], BF16, name="g_raw%d" % p)
+            i, j = g_place[p]
             for h in range(2):
-                nc.sync.dma_start(out=g_p[h:PARTS:2], in_=g_view[h, p])
-            g_raw.append(g_p[:].rearrange("p (w q k) -> p w q k", w=PACK, q=SIDE))
-        x_raw = []
-        for u in range(SIDE):
-            x_u = keep.tile([PARTS, SIDE, PACK * C], BF16, name="x_raw%d" % u)
-            nc.sync.dma_start(out=x_u[:], in_=x_view[:, SIDE * u : SIDE * (u + 1), :])
-            x_raw.append(x_u)
+                nc.sync.dma_start(out=g_tiles[i][h:PARTS:2, j], in_=g_view[h, p])
+        g_views = [t[:].rearrange("p n (w q k) -> p n w q k", w=PACK, q=SIDE) for t in g_tiles]
+        x_raw = keep.tile([PARTS, SIDE * SIDE, PACK * C], BF16, name="x_raw")
+        for v in range(SIDE):
+            nc.sync.dma_start(out=x_raw[:, SIDE * v : SIDE * (v + 1), :], in_=x_view[:, v])
+
+        warm = keep.tile([PARTS, 2], F32, name="warm")
+        nc.vector.memset(warm[:, 0:1], 0.0)
+        nc.scalar.activation(out=warm[:, 1:2], in_=warm[:, 0:1], func=COPY, scale=1.0)
 
         gy_width = (PAD_BLOCKS + SIDE * SIDE) * K
         gy_codes = keep.tile([PARTS, gy_width], U32, name="gy_codes", align_bytes=64)
@@ -75,17 +77,20 @@ def tile_iwht3layer_pa_s_kernel(tc, trans, weight, bias, grad_out, out):
         both = ((0, ADD), (1, SUB))
 
         g_f32 = [
-            keep.tile([PARTS, SIDE, SLOTS, PACK, SLOT], F32, name="g_f32_%d" % p) for p in range(SIDE)
+            [keep.tile([PARTS, SIDE, PACK, SLOT], F32, name="g_f32_%d_%d" % (s, p)) for p in range(SIDE)]
+            for s in range(SLOTS)
         ]
         turned = [
             [keep.tile([PARTS, SIDE, PARTS], F32, name="turned%d_%d" % (s, v)) for v in range(SIDE)]
             for s in range(SLOTS)
         ]
+        half_sums = [keep.tile([PARTS, SIDE, SLOT, PACK], F32, name="half_sum%d" % s) for s in range(SLOTS)]
 
-        def cast(p, s):
+        def cast(s, p):
+            i, j = g_place[p]
             nc.scalar.activation(
-                out=g_f32[p][:, :, s],
-                in_=g_raw[p][:, :, :, SLOT * s : SLOT * (s + 1)].rearrange("p w q e -> p q w e"),
+                out=g_f32[s][p][:],
+                in_=g_views[i][:, j, :, :, SLOT * s : SLOT * (s + 1)].rearrange("p w q e -> p q w e"),
                 func=COPY,
                 scale=4.0,
             )
@@ -101,58 +106,55 @@ def tile_iwht3layer_pa_s_kernel(tc, trans, weight, bias, grad_out, out):
                     stop=(i == len(terms) - 1),
                 )
 
-        def new_bank(shape):
-            return flip.tile(shape, F32, name="bank", tag="bank")
+        def new_banks():
+            return [psum.tile([PARTS, SIDE, PARTS], F32, name="bank", tag="bank") for g in range(SIDE)]
 
-        def turn_q(bank, s, p, g):
-            add_up(bank[:, p, :], [g_f32[p][:, q, s].rearrange("p w e -> p (w e)") for q in PLUS[g]])
+        def turn_q(banks, s, p, g):
+            add_up(banks[g][:, p, :], [g_f32[s][p][:, q].rearrange("p w e -> p (w e)") for q in PLUS[g]])
 
-        def half_out_q(bank, s):
-            nc.scalar.activation(out=turned[s][0][:], in_=bank[:], func=COPY, scale=0.5)
+        def half_out_q(banks, s):
+            nc.scalar.activation(out=turned[s][0][:], in_=banks[0][:], func=COPY, scale=0.5)
 
-        def rest_out_q(bank, s, v):
-            nc.vector.tensor_tensor(out=turned[s][v][:], in0=bank[:], in1=turned[s][0][:], op=SUB)
+        def rest_out_q(banks, s):
+            for v in range(1, SIDE):
+                nc.vector.tensor_tensor(out=turned[s][v][:], in0=banks[v][:], in1=turned[s][0][:], op=SUB)
 
-        def turn_p(pair, g):
-            bank = new_bank([PARTS, 2, SLOTS, PARTS])
-            for a in range(2):
-                for s in range(SLOTS):
-                    add_up(bank[:, a, s, :], [turned[s][2 * pair + a][:, p, :] for p in PLUS[g]])
-            return bank
+        def turn_p(banks, s):
+            for g in range(SIDE):
+                for v in range(SIDE):
+                    add_up(banks[g][:, v, :], [turned[s][v][:, p, :] for p in PLUS[g]])
 
-        def half_out_p(bank, pair):
-            half_sum = keep.tile([PARTS, 2, K_PE, PACK], F32, name="half_sum%d" % pair)
+        def half_out_p(banks, s):
             nc.scalar.activation(
-                out=half_sum[:].rearrange("p a (s e) w -> p a s e w", s=SLOTS),
-                in_=bank[:].rearrange("p a s (w e) -> p a s e w", w=PACK),
+                out=half_sums[s][:],
+                in_=banks[0][:].rearrange("p v (w e) -> p v e w", w=PACK),
                 func=COPY,
                 scale=0.5,
             )
             nc.scalar.copy(
-                out=gy_by_place[:, BLOCK_OF_U[0], 2 * pair : 2 * pair + 2, 0:K_PE, :], in_=half_sum[:]
+                out=gy_by_place[:, BLOCK_OF_U[0], :, SLOT * s : SLOT * (s + 1), :], in_=half_sums[s][:]
             )
-            return half_sum
 
-        def rest_out_p(bank, half_sum, pair, u):
-            nc.vector.tensor_tensor(
-                out=gy_by_place[:, BLOCK_OF_U[u], 2 * pair : 2 * pair + 2, 0:K_PE, :].rearrange(
-                    "p a (s e) w -> p a s e w", s=SLOTS
-                ),
-                in0=bank[:].rearrange("p a s (w e) -> p a s e w", w=PACK),
-                in1=half_sum[:].rearrange("p a (s e) w -> p a s e w", s=SLOTS),
-                op=SUB,
-            )
+        def rest_out_p(banks, s):
+            for u in (2, 1, 3):
+                nc.vector.tensor_tensor(
+                    out=gy_by_place[:, BLOCK_OF_U[u], :, SLOT * s : SLOT * (s + 1), :],
+                    in0=banks[u][:].rearrange("p v (w e) -> p v e w", w=PACK),
+                    in1=half_sums[s][:],
+                    op=SUB,
+                )
 
         half_q = [keep.tile([PARTS, SIDE, PACK, 2, K_VE], F32, name="half_q%d" % a) for a in range(2)]
         done_q = [keep.tile([PARTS, 2, SIDE, PACK, K_VE], F32, name="done_q%d" % a) for a in range(2)]
         half_p = [keep.tile([PARTS, 2, 2, PACK, 2, K_VE], F32, name="half_p%d" % a) for a in range(2)]
 
-        def step_q1(p):
+        def step_q1(i):
+            rows = [p for p in range(SIDE) if g_place[p][0] == i]
             for v1, op in both:
                 nc.vector.tensor_tensor(
-                    out=half_q[v1][:, p],
-                    in0=g_raw[p][:, :, 0:2, K_PE:K],
-                    in1=g_raw[p][:, :, 2:4, K_PE:K],
+                    out=half_q[v1][:, rows[0] : rows[-1] + 1],
+                    in0=g_views[i][:, :, :, 0:2, K_PE:K],
+                    in1=g_views[i][:, :, :, 2:4, K_PE:K],
                     op=op,
                 )
 
@@ -171,7 +173,17 @@ def tile_iwht3layer_pa_s_kernel(tc, trans, weight, bias, grad_out, out):
             for u1, op in both:
                 nc.vector.tensor_tensor(out=dst[:, u1], in0=src[:, 0], in1=src[:, 1], op=op)
 
-        def step_p0(v, u0):
+        gy_by_bits = gy_grouped[:].rearrange("p (c v b a) k w -> p c b v a k w", c=2, v=2, b=2)
+
+        def step_p0(v1, u0):
+            nc.vector.tensor_tensor(
+                out=gy_by_bits[:, v1, u0, :, :, K_PE:K, :],
+                in0=half_p[v1][:, :, 0].rearrange("p v w a k -> p v a k w"),
+                in1=half_p[v1][:, :, 1].rearrange("p v w a k -> p v a k w"),
+                op=both[u0][1],
+            )
+
+        def step_p0_one(v, u0):
             src = half_p[v // 2][:, v % 2]
             first = SIDE * v + 2 * u0
             nc.vector.tensor_tensor(
@@ -181,42 +193,45 @@ def tile_iwht3layer_pa_s_kernel(tc, trans, weight, bias, grad_out, out):
                 op=both[u0][1],
             )
 
-        x_grouped = [
-            keep.tile([PARTS, SIDE, C, PACK], BF16, name="x_grouped%d" % u, align_bytes=64)
-            for u in range(SIDE)
-        ]
-        x_codes = [keep.tile([PARTS, SIDE, C], U32, name="x_codes%d" % u, align_bytes=64) for u in range(SIDE)]
-        x_scales = [keep.tile([PARTS, SIDE, C], U8, name="x_scales%d" % u, align_bytes=64) for u in range(SIDE)]
+        x_grouped = keep.tile([PARTS, SIDE * SIDE, C, PACK], BF16, name="x_grouped", align_bytes=64)
+        x_codes = keep.tile([PARTS, SIDE * SIDE, C], U32, name="x_codes", align_bytes=64)
+        x_scales = keep.tile([PARTS, SIDE * SIDE, C], U8, name="x_scales", align_bytes=64)
 
-        def regroup(u, v):
-            nc.scalar.copy(
-                out=x_grouped[u][:, v].rearrange("p (r e) w -> p r w e", e=RUN),
-                in_=x_raw[u][:, v].rearrange("p (w r e) -> p r w e", w=PACK, e=RUN),
-            )
+        def regroup(v):
+            for t in range(SIDE * v, SIDE * (v + 1)):
+                nc.scalar.copy(
+                    out=x_grouped[:, t].rearrange("p (r e) w -> p r w e", e=RUN),
+                    in_=x_raw[:, t].rearrange("p (w r e) -> p r w e", w=PACK, e=RUN),
+                )
 
-        def quantise_x(u):
+        def quantise_x(v):
+            start = SIDE * v
+            stop = SIDE * (v + 1)
             nc.vector.quantize_mx(
-                out=x_codes[u][:].rearrange("p v c -> p (v c)").bitcast(E4M3_X4),
-                scales=x_scales[u][:].rearrange("p v c -> p (v c)"),
-                in_=x_grouped[u][:].rearrange("p v c w -> p (v c w)"),
+                out=x_codes[:, start:stop].rearrange("p t c -> p (t c)").bitcast(E4M3_X4),
+                scales=x_scales[:, start:stop].rearrange("p t c -> p (t c)"),
+                in_=x_grouped[:, start:stop].rearrange("p t c w -> p (t c w)"),
             )
 
-        def finish(v, u0):
-            first = SIDE * v + 2 * u0
-            fresh = slice((PAD_BLOCKS + first) * K, (PAD_BLOCKS + first + 2) * K)
+        def quantise_gy(first, count):
+            fresh = slice((PAD_BLOCKS + first) * K, (PAD_BLOCKS + first + count) * K)
             nc.vector.quantize_mx(
                 out=gy_codes[:, fresh].bitcast(E5M2_X4),
                 scales=gy_scales[:, fresh],
-                in_=gy_grouped[:, first : first + 2].rearrange("p a k w -> p (a k w)"),
+                in_=gy_grouped[:, first : first + count].rearrange("p a k w -> p (a k w)"),
             )
+
+        def multiply(v, u0):
+            first = SIDE * v + 2 * u0
             result = outs.tile([PARTS, 2, K], F32, name="result", tag="result")
             for u1 in range(2):
                 window = slice((first + u1) * K, (first + u1) * K + N_PASS)
-                acc = accs.tile([PARTS, N_PASS], F32, name="acc", tag="acc")
+                acc = psum.tile([PARTS, N_PASS], F32, name="acc", tag="bank")
+                t = SIDE * v + 2 * u1 + u0
                 nc.tensor.matmul_mx(
                     out=acc[:],
-                    lhsT=x_codes[2 * u1 + u0][:, v, :].bitcast(E4M3_X4),
-                    lhsT_scale=x_scales[2 * u1 + u0][:, v, :],
+                    lhsT=x_codes[:, t, :].bitcast(E4M3_X4),
+                    lhsT_scale=x_scales[:, t, :],
                     rhs=gy_codes[:, window].bitcast(E5M2_X4),
                     rhs_scale=gy_scales[:, window],
                     start=True,
@@ -230,60 +245,57 @@ def tile_iwht3layer_pa_s_kernel(tc, trans, weight, bias, grad_out, out):
                 )
             nc.sync.dma_start(out=out_view[:, v, u0], in_=result[:])
 
-        def regroup_range(start, stop):
-            for t in range(start, stop):
-                regroup(t // SIDE, t % SIDE)
-
-        first_banks = [new_bank([PARTS, SIDE, PARTS]) for g in range(SIDE)]
+        banks_q0 = new_banks()
         for p in range(SIDE):
-            cast(p, 0)
-            cast(p, 1)
+            cast(0, p)
+            cast(1, p)
             step_q1(p)
             for g in range(SIDE):
-                turn_q(first_banks[g], 0, p, g)
-        regroup_range(0, 1)
-        half_out_q(first_banks[0], 0)
+                turn_q(banks_q0, 0, p, g)
+        half_out_q(banks_q0, 0)
+        banks_q1 = new_banks()
+        for g in range(SIDE):
+            for p in range(SIDE):
+                turn_q(banks_q1, 1, p, g)
         step_q0(0)
-        step_q0(1)
-        second_banks = []
-        for g in range(2):
-            second_banks.append(new_bank([PARTS, SIDE, PARTS]))
-            for p in range(SIDE):
-                turn_q(second_banks[g], 1, p, g)
-        regroup_range(1, 5)
-        half_out_q(second_banks[0], 1)
-        for v in range(1, SIDE):
-            rest_out_q(first_banks[v], 0, v)
-        for g in range(2, SIDE):
-            second_banks.append(new_bank([PARTS, SIDE, PARTS]))
-            for p in range(SIDE):
-                turn_q(second_banks[g], 1, p, g)
-        for v in range(1, SIDE):
-            rest_out_q(second_banks[v], 1, v)
-
-        banks = [turn_p(0, g) for g in range(SIDE)]
-        regroup_range(5, SIDE * SIDE)
+        rest_out_q(banks_q0, 0)
+        banks_p0 = new_banks()
+        turn_p(banks_p0, 0)
+        half_out_q(banks_q1, 1)
+        regroup(0)
         step_p1(0)
+        rest_out_q(banks_q1, 1)
+        banks_p1 = new_banks()
+        turn_p(banks_p1, 1)
+        half_out_p(banks_p0, 0)
+        regroup(1)
+        half_out_p(banks_p1, 1)
+        regroup(2)
+        regroup(3)
+        step_p0(0, 0)
+        step_p0(0, 1)
+        rest_out_p(banks_p0, 0)
+        rest_out_p(banks_p1, 1)
+        quantise_x(0)
+        quantise_gy(0, 4)
+        multiply(0, 0)
+        multiply(0, 1)
+        step_q0(1)
+        quantise_x(1)
+        quantise_gy(4, 4)
+        multiply(1, 0)
+        multiply(1, 1)
         step_p1(1)
-        for v in range(2):
-            for u0 in range(2):
-                step_p0(v, u0)
-        half_sum = half_out_p(banks[0], 0)
-        for u in (2, 1, 3):
-            rest_out_p(banks[u], half_sum, 0, u)
-
-        banks = [turn_p(1, g) for g in range(SIDE)]
-        half_sum = half_out_p(banks[0], 1)
-        for u in range(SIDE):
-            quantise_x(u)
-        for v in range(2):
-            for u0 in range(2):
-                finish(v, u0)
-        for v in range(2, SIDE):
-            for u0 in range(2):
-                step_p0(v, u0)
-        for u in (2, 1, 3):
-            rest_out_p(banks[u], half_sum, 1, u)
-        for v in range(2, SIDE):
-            for u0 in range(2):
-                finish(v, u0)
+        quantise_x(2)
+        step_p0_one(2, 0)
+        step_p0_one(2, 1)
+        quantise_x(3)
+        quantise_gy(8, 4)
+        multiply(2, 0)
+        multiply(2, 1)
+        step_p0_one(3, 0)
+        step_p0_one(3, 1)
+        quantise_gy(12, 2)
+        multiply(3, 0)
+        quantise_gy(14, 2)
+        multiply(3, 1)

@@ -30,6 +30,7 @@ SLOTS = 2
 K_PE = SLOT * SLOTS
 K_VE = K - K_PE
 PLUS = ((0, 1, 2, 3), (0, 2), (0, 1), (0, 3))
+SPLIT_LOADS = (0, 3)
 BLOCK_OF_U = (0, 2, 1, 3)
 
 
@@ -53,10 +54,13 @@ def tile_iwht3layer_pa_s_kernel(tc, trans, weight, bias, grad_out, out):
 
         g_tiles = [keep.tile([PARTS, 1, PACK * SIDE * K], BF16, name="g_raw%d" % p) for p in range(SIDE)]
         g_place = ((0, 0), (1, 0), (2, 0), (3, 0))
+        half_row = PACK * SIDE * K // 2
         for p in range(SIDE):
             i, j = g_place[p]
-            for h in range(2):
-                nc.sync.dma_start(out=g_tiles[i][h:PARTS:2, j], in_=g_view[h, p])
+            cuts = (0, half_row, 2 * half_row) if p in SPLIT_LOADS else (0, 2 * half_row)
+            for a, b in zip(cuts[0:-1], cuts[1:]):
+                for h in range(2):
+                    nc.sync.dma_start(out=g_tiles[i][h:PARTS:2, j, a:b], in_=g_view[h, p][:, a:b])
         g_views = [t[:].rearrange("p n (w q k) -> p n w q k", w=PACK, q=SIDE) for t in g_tiles]
         x_raw = keep.tile([PARTS, SIDE * SIDE, PACK * C], BF16, name="x_raw")
         for v in range(SIDE):
@@ -148,15 +152,16 @@ def tile_iwht3layer_pa_s_kernel(tc, trans, weight, bias, grad_out, out):
         done_q = [keep.tile([PARTS, 2, SIDE, PACK, K_VE], F32, name="done_q%d" % a) for a in range(2)]
         half_p = [keep.tile([PARTS, 2, 2, PACK, 2, K_VE], F32, name="half_p%d" % a) for a in range(2)]
 
-        def step_q1(i):
-            rows = [p for p in range(SIDE) if g_place[p][0] == i]
-            for v1, op in both:
-                nc.vector.tensor_tensor(
-                    out=half_q[v1][:, rows[0] : rows[-1] + 1],
-                    in0=g_views[i][:, :, :, 0:2, K_PE:K],
-                    in1=g_views[i][:, :, :, 2:4, K_PE:K],
-                    op=op,
-                )
+        def step_q1(p):
+            cuts = (0, PACK // 2, PACK) if p in SPLIT_LOADS else (0, PACK)
+            for a, b in zip(cuts[0:-1], cuts[1:]):
+                for v1, op in both:
+                    nc.vector.tensor_tensor(
+                        out=half_q[v1][:, p, a:b],
+                        in0=g_views[p][:, 0, a:b, 0:2, K_PE:K],
+                        in1=g_views[p][:, 0, a:b, 2:4, K_PE:K],
+                        op=op,
+                    )
 
         def step_q0(v1):
             for v0, op in both:
@@ -167,21 +172,10 @@ def tile_iwht3layer_pa_s_kernel(tc, trans, weight, bias, grad_out, out):
                     op=op,
                 )
 
-        def step_p1(v1):
+        def step_p1(v1, u1):
             src = done_q[v1][:].rearrange("p v (a b) w k -> p a v (b w) k", a=2)
             dst = half_p[v1][:].rearrange("p v b w a k -> p a v (b w) k")
-            for u1, op in both:
-                nc.vector.tensor_tensor(out=dst[:, u1], in0=src[:, 0], in1=src[:, 1], op=op)
-
-        gy_by_bits = gy_grouped[:].rearrange("p (c v b a) k w -> p c b v a k w", c=2, v=2, b=2)
-
-        def step_p0(v1, u0):
-            nc.vector.tensor_tensor(
-                out=gy_by_bits[:, v1, u0, :, :, K_PE:K, :],
-                in0=half_p[v1][:, :, 0].rearrange("p v w a k -> p v a k w"),
-                in1=half_p[v1][:, :, 1].rearrange("p v w a k -> p v a k w"),
-                op=both[u0][1],
-            )
+            nc.vector.tensor_tensor(out=dst[:, u1], in0=src[:, 0], in1=src[:, 1], op=both[u1][1])
 
         def step_p0_one(v, u0):
             src = half_p[v // 2][:, v % 2]
@@ -221,8 +215,9 @@ def tile_iwht3layer_pa_s_kernel(tc, trans, weight, bias, grad_out, out):
                 in_=gy_grouped[:, first : first + count].rearrange("p a k w -> p (a k w)"),
             )
 
-        def multiply(v, u0):
+        def finish(v, u0):
             first = SIDE * v + 2 * u0
+            quantise_gy(first, 2)
             result = outs.tile([PARTS, 2, K], F32, name="result", tag="result")
             for u1 in range(2):
                 window = slice((first + u1) * K, (first + u1) * K + N_PASS)
@@ -243,7 +238,8 @@ def tile_iwht3layer_pa_s_kernel(tc, trans, weight, bias, grad_out, out):
                     func=COPY,
                     scale=1.0 / (SIDE * SIDE),
                 )
-            nc.sync.dma_start(out=out_view[:, v, u0], in_=result[:])
+            queue = nc.scalar if (v, u0) == (SIDE - 1, 1) else nc.sync
+            queue.dma_start(out=out_view[:, v, u0], in_=result[:])
 
         banks_q0 = new_banks()
         for p in range(SIDE):
@@ -263,7 +259,8 @@ def tile_iwht3layer_pa_s_kernel(tc, trans, weight, bias, grad_out, out):
         turn_p(banks_p0, 0)
         half_out_q(banks_q1, 1)
         regroup(0)
-        step_p1(0)
+        step_p1(0, 0)
+        step_p1(0, 1)
         rest_out_q(banks_q1, 1)
         banks_p1 = new_banks()
         turn_p(banks_p1, 1)
@@ -272,30 +269,28 @@ def tile_iwht3layer_pa_s_kernel(tc, trans, weight, bias, grad_out, out):
         half_out_p(banks_p1, 1)
         regroup(2)
         regroup(3)
-        step_p0(0, 0)
-        step_p0(0, 1)
+        step_p0_one(0, 0)
+        step_p0_one(0, 1)
+        step_q0(1)
         rest_out_p(banks_p0, 0)
         rest_out_p(banks_p1, 1)
         quantise_x(0)
-        quantise_gy(0, 4)
-        multiply(0, 0)
-        multiply(0, 1)
-        step_q0(1)
+        finish(0, 0)
+        step_p0_one(1, 0)
         quantise_x(1)
-        quantise_gy(4, 4)
-        multiply(1, 0)
-        multiply(1, 1)
-        step_p1(1)
+        finish(0, 1)
+        step_p0_one(1, 1)
+        step_p1(1, 0)
+        finish(1, 0)
+        step_p1(1, 1)
         quantise_x(2)
+        finish(1, 1)
         step_p0_one(2, 0)
         step_p0_one(2, 1)
-        quantise_x(3)
-        quantise_gy(8, 4)
-        multiply(2, 0)
-        multiply(2, 1)
+        finish(2, 0)
         step_p0_one(3, 0)
+        finish(2, 1)
+        quantise_x(3)
         step_p0_one(3, 1)
-        quantise_gy(12, 2)
-        multiply(3, 0)
-        quantise_gy(14, 2)
-        multiply(3, 1)
+        finish(3, 0)
+        finish(3, 1)

@@ -172,15 +172,17 @@ def tile_iwht3layer_pa_s_kernel(tc, trans, weight, bias, grad_out, out):
                     op=op,
                 )
 
-        def step_p1(v1, u1):
+        def step_p1(engine, v1, u1, some):
             src = done_q[v1][:].rearrange("p v (a b) w k -> p a v (b w) k", a=2)
             dst = half_p[v1][:].rearrange("p v b w a k -> p a v (b w) k")
-            nc.vector.tensor_tensor(out=dst[:, u1], in0=src[:, 0], in1=src[:, 1], op=both[u1][1])
+            engine.tensor_tensor(
+                out=dst[:, u1, some], in0=src[:, 0, some], in1=src[:, 1, some], op=both[u1][1]
+            )
 
-        def step_p0_one(v, u0):
+        def step_p0_one(v, u0, engine=nc.vector):
             src = half_p[v // 2][:, v % 2]
             first = SIDE * v + 2 * u0
-            nc.vector.tensor_tensor(
+            engine.tensor_tensor(
                 out=gy_grouped[:, first : first + 2, K_PE:K, :],
                 in0=src[:, 0].rearrange("p w a k -> p a k w"),
                 in1=src[:, 1].rearrange("p w a k -> p a k w"),
@@ -253,14 +255,19 @@ def tile_iwht3layer_pa_s_kernel(tc, trans, weight, bias, grad_out, out):
         for g in range(SIDE):
             for p in range(SIDE):
                 turn_q(banks_q1, 1, p, g)
+        low = slice(0, 1)
+        high = slice(1, 2)
+        whole = slice(0, 2)
         step_q0(0)
+        step_p1(nc.gpsimd, 0, 0, high)
         rest_out_q(banks_q0, 0)
         banks_p0 = new_banks()
         turn_p(banks_p0, 0)
         half_out_q(banks_q1, 1)
         regroup(0)
-        step_p1(0, 0)
-        step_p1(0, 1)
+        step_p1(nc.vector, 0, 0, low)
+        step_p1(nc.vector, 0, 1, whole)
+        step_p0_one(1, 1, nc.gpsimd)
         rest_out_q(banks_q1, 1)
         banks_p1 = new_banks()
         turn_p(banks_p1, 1)
@@ -272,6 +279,8 @@ def tile_iwht3layer_pa_s_kernel(tc, trans, weight, bias, grad_out, out):
         step_p0_one(0, 0)
         step_p0_one(0, 1)
         step_q0(1)
+        step_p1(nc.gpsimd, 1, 0, high)
+        step_p1(nc.gpsimd, 1, 1, high)
         rest_out_p(banks_p0, 0)
         rest_out_p(banks_p1, 1)
         quantise_x(0)
@@ -279,10 +288,9 @@ def tile_iwht3layer_pa_s_kernel(tc, trans, weight, bias, grad_out, out):
         step_p0_one(1, 0)
         quantise_x(1)
         finish(0, 1)
-        step_p0_one(1, 1)
-        step_p1(1, 0)
+        step_p1(nc.vector, 1, 0, low)
         finish(1, 0)
-        step_p1(1, 1)
+        step_p1(nc.vector, 1, 1, low)
         quantise_x(2)
         finish(1, 1)
         step_p0_one(2, 0)

@@ -30,7 +30,7 @@ SLOTS = 2
 K_PE = SLOT * SLOTS
 K_VE = K - K_PE
 PLUS = ((0, 1, 2, 3), (0, 2), (0, 1), (0, 3))
-SPLIT_LOADS = (0, 3)
+SPLIT_LOADS = ()
 BLOCK_OF_U = (0, 2, 1, 3)
 
 
@@ -240,8 +240,7 @@ def tile_iwht3layer_pa_s_kernel(tc, trans, weight, bias, grad_out, out):
                     func=COPY,
                     scale=1.0 / (SIDE * SIDE),
                 )
-            queue = nc.scalar if (v, u0) == (SIDE - 1, 1) else nc.sync
-            queue.dma_start(out=out_view[:, v, u0], in_=result[:])
+            nc.sync.dma_start(out=out_view[:, v, u0], in_=result[:])
 
         banks_q0 = new_banks()
         for p in range(SIDE):

@@ -31,7 +31,8 @@ K_PE = SLOT * SLOTS
 K_VE = K - K_PE
 PLUS = ((0, 1, 2, 3), (0, 2), (0, 1), (0, 3))
 SPLIT_LOADS = ()
-BLOCK_OF_U = (0, 2, 1, 3)
+PAIRS = 8
+PAIR_COLS = 2 * K
 
 
 def tile_iwht3layer_pa_s_kernel(tc, trans, weight, bias, grad_out, out):
@@ -70,14 +71,14 @@ def tile_iwht3layer_pa_s_kernel(tc, trans, weight, bias, grad_out, out):
         nc.vector.memset(warm[:, 0:1], 0.0)
         nc.scalar.activation(out=warm[:, 1:2], in_=warm[:, 0:1], func=COPY, scale=1.0)
 
-        gy_width = (PAD_BLOCKS + SIDE * SIDE) * K
+        gy_width = (1 + PAIRS) * PAIR_COLS
         gy_codes = keep.tile([PARTS, gy_width], U32, name="gy_codes", align_bytes=64)
         gy_scales = keep.tile([PARTS, gy_width], U8, name="gy_scales", align_bytes=64)
-        nc.vector.memset(gy_codes[:, 0 : PAD_BLOCKS * K].bitcast(I32), 0)
-        nc.vector.memset(gy_scales[:, 0 : PAD_BLOCKS * K].bitcast(I32), 0)
+        nc.vector.memset(gy_codes[:, 0:PAIR_COLS].bitcast(I32), 0)
+        nc.vector.memset(gy_scales[:, 0:PAIR_COLS].bitcast(I32), 0)
 
-        gy_grouped = keep.tile([PARTS, SIDE * SIDE, K, PACK], BF16, name="gy_grouped", align_bytes=64)
-        gy_by_place = gy_grouped[:].rearrange("p (v b) k w -> p b v k w", b=SIDE)
+        gy_grouped = keep.tile([PARTS, PAIRS, 2, 2, K_PE, PACK], BF16, name="gy_grouped", align_bytes=64)
+        gy_by_place = gy_grouped[:].rearrange("p (v b) h a k w -> p b h a v k w", b=2)
         both = ((0, ADD), (1, SUB))
 
         g_f32 = [
@@ -136,13 +137,13 @@ def tile_iwht3layer_pa_s_kernel(tc, trans, weight, bias, grad_out, out):
                 scale=0.5,
             )
             nc.scalar.copy(
-                out=gy_by_place[:, BLOCK_OF_U[0], :, SLOT * s : SLOT * (s + 1), :], in_=half_sums[s][:]
+                out=gy_by_place[:, 0, 0, 0, :, SLOT * s : SLOT * (s + 1), :], in_=half_sums[s][:]
             )
 
         def rest_out_p(banks, s):
             for u in (2, 1, 3):
                 nc.vector.tensor_tensor(
-                    out=gy_by_place[:, BLOCK_OF_U[u], :, SLOT * s : SLOT * (s + 1), :],
+                    out=gy_by_place[:, u % 2, 0, u // 2, :, SLOT * s : SLOT * (s + 1), :],
                     in0=banks[u][:].rearrange("p v (w e) -> p v e w", w=PACK),
                     in1=half_sums[s][:],
                     op=SUB,
@@ -179,15 +180,23 @@ def tile_iwht3layer_pa_s_kernel(tc, trans, weight, bias, grad_out, out):
                 out=dst[:, u1, some], in0=src[:, 0, some], in1=src[:, 1, some], op=both[u1][1]
             )
 
-        def step_p0_one(v, u0, engine=nc.vector):
+        def step_p0_one(v, u0, on_gpsimd=False):
             src = half_p[v // 2][:, v % 2]
-            first = SIDE * v + 2 * u0
-            engine.tensor_tensor(
-                out=gy_grouped[:, first : first + 2, K_PE:K, :],
-                in0=src[:, 0].rearrange("p w a k -> p a k w"),
-                in1=src[:, 1].rearrange("p w a k -> p a k w"),
-                op=both[u0][1],
-            )
+            dst = gy_grouped[:, 2 * v + u0, 1]
+            if not on_gpsimd:
+                nc.vector.tensor_tensor(
+                    out=dst.rearrange("p a (r e) w -> p (a r) w e", e=RUN),
+                    in0=src[:, 0].rearrange("p w a (r e) -> p (a r) w e", e=RUN),
+                    in1=src[:, 1].rearrange("p w a (r e) -> p (a r) w e", e=RUN),
+                    op=both[u0][1],
+                )
+            else:
+                nc.gpsimd.tensor_tensor(
+                    out=dst,
+                    in0=src[:, 0].rearrange("p w a k -> p a k w"),
+                    in1=src[:, 1].rearrange("p w a k -> p a k w"),
+                    op=both[u0][1],
+                )
 
         x_grouped = keep.tile([PARTS, SIDE * SIDE, C, PACK], BF16, name="x_grouped", align_bytes=64)
         x_codes = keep.tile([PARTS, SIDE * SIDE, C], U32, name="x_codes", align_bytes=64)
@@ -209,20 +218,17 @@ def tile_iwht3layer_pa_s_kernel(tc, trans, weight, bias, grad_out, out):
                 in_=x_grouped[:, start:stop].rearrange("p t c w -> p (t c w)"),
             )
 
-        def quantise_gy(first, count):
-            fresh = slice((PAD_BLOCKS + first) * K, (PAD_BLOCKS + first + count) * K)
+        def finish(v, u0):
+            pair = 2 * v + u0
+            fresh = slice((1 + pair) * PAIR_COLS, (2 + pair) * PAIR_COLS)
             nc.vector.quantize_mx(
                 out=gy_codes[:, fresh].bitcast(E5M2_X4),
                 scales=gy_scales[:, fresh],
-                in_=gy_grouped[:, first : first + count].rearrange("p a k w -> p (a k w)"),
+                in_=gy_grouped[:, pair].rearrange("p h a k w -> p (h a k w)"),
             )
-
-        def finish(v, u0):
-            first = SIDE * v + 2 * u0
-            quantise_gy(first, 2)
+            window = slice(pair * PAIR_COLS, pair * PAIR_COLS + N_PASS)
             result = outs.tile([PARTS, 2, K], F32, name="result", tag="result")
             for u1 in range(2):
-                window = slice((first + u1) * K, (first + u1) * K + N_PASS)
                 acc = psum.tile([PARTS, N_PASS], F32, name="acc", tag="bank")
                 t = SIDE * v + 2 * u1 + u0
                 nc.tensor.matmul_mx(
@@ -235,8 +241,8 @@ def tile_iwht3layer_pa_s_kernel(tc, trans, weight, bias, grad_out, out):
                     stop=True,
                 )
                 nc.scalar.activation(
-                    out=result[:, u1, :],
-                    in_=acc[:, N_PASS - K : N_PASS],
+                    out=result[:, u1, :].rearrange("p (h k) -> p h k", h=2),
+                    in_=acc[:, N_PASS - PAIR_COLS : N_PASS].rearrange("p (h a k) -> p a h k", h=2, a=2)[:, u1],
                     func=COPY,
                     scale=1.0 / (SIDE * SIDE),
                 )
@@ -266,7 +272,7 @@ def tile_iwht3layer_pa_s_kernel(tc, trans, weight, bias, grad_out, out):
         regroup(0)
         step_p1(nc.vector, 0, 0, low)
         step_p1(nc.vector, 0, 1, whole)
-        step_p0_one(1, 1, nc.gpsimd)
+        step_p0_one(1, 1, True)
         rest_out_q(banks_q1, 1)
         banks_p1 = new_banks()
         turn_p(banks_p1, 1)

@@ -209,9 +209,9 @@ def tile_iwht3layer_pa_s_kernel(tc, trans, weight, bias, grad_out, out):
                     in_=x_raw[:, t].rearrange("p (w r e) -> p r w e", w=PACK, e=RUN),
                 )
 
-        def quantise_x(v):
+        def quantise_x(v, count):
             start = SIDE * v
-            stop = SIDE * (v + 1)
+            stop = SIDE * (v + count)
             nc.vector.quantize_mx(
                 out=x_codes[:, start:stop].rearrange("p t c -> p (t c)").bitcast(E4M3_X4),
                 scales=x_scales[:, start:stop].rearrange("p t c -> p (t c)"),
@@ -270,6 +270,7 @@ def tile_iwht3layer_pa_s_kernel(tc, trans, weight, bias, grad_out, out):
         turn_p(banks_p0, 0)
         half_out_q(banks_q1, 1)
         regroup(0)
+        regroup(1)
         step_p1(nc.vector, 0, 0, low)
         step_p1(nc.vector, 0, 1, whole)
         step_p0_one(1, 1, True)
@@ -277,33 +278,30 @@ def tile_iwht3layer_pa_s_kernel(tc, trans, weight, bias, grad_out, out):
         banks_p1 = new_banks()
         turn_p(banks_p1, 1)
         half_out_p(banks_p0, 0)
-        regroup(1)
         half_out_p(banks_p1, 1)
         regroup(2)
         regroup(3)
         step_p0_one(0, 0)
         step_p0_one(0, 1)
+        step_p0_one(1, 0)
+        quantise_x(0, 2)
         step_q0(1)
         step_p1(nc.gpsimd, 1, 0, high)
         step_p1(nc.gpsimd, 1, 1, high)
         rest_out_p(banks_p0, 0)
         rest_out_p(banks_p1, 1)
-        quantise_x(0)
         finish(0, 0)
-        step_p0_one(1, 0)
-        quantise_x(1)
-        finish(0, 1)
         step_p1(nc.vector, 1, 0, low)
-        finish(1, 0)
+        finish(0, 1)
         step_p1(nc.vector, 1, 1, low)
-        quantise_x(2)
+        finish(1, 0)
+        quantise_x(2, 2)
         finish(1, 1)
         step_p0_one(2, 0)
         step_p0_one(2, 1)
         finish(2, 0)
         step_p0_one(3, 0)
         finish(2, 1)
-        quantise_x(3)
         step_p0_one(3, 1)
         finish(3, 0)
         finish(3, 1)

@@ -28,9 +28,14 @@ PAD_BLOCKS = N_PASS // K - 1
 SLOT = PARTS // PACK
 SLOTS = 2
 K_PE = SLOT * SLOTS
-K_VE = K - K_PE
+K_MM = 12
+MM_STEPS = K_MM // 2
+MM_HALF = MM_STEPS // 2
+K_VE = K - K_PE - K_MM
+K_TOP = K_PE + K_VE
+K_ROW = 56
+PIXELS = SIDE * PACK * SIDE
 PLUS = ((0, 1, 2, 3), (0, 2), (0, 1), (0, 3))
-SPLIT_LOADS = ()
 PAIRS = 8
 PAIR_COLS = 2 * K
 
@@ -48,21 +53,21 @@ def tile_iwht3layer_pa_s_kernel(tc, trans, weight, bias, grad_out, out):
         ctx.enter_context(tc.manual_schedule())
         keep = ctx.enter_context(tc.tile_pool(name="keep", bufs=1))
         outs = ctx.enter_context(tc.tile_pool(name="outs", bufs=4))
-        psum = ctx.enter_context(tc.psum_pool(name="psum", bufs=8))
+        psum = ctx.enter_context(tc.psum_pool(name="psum", bufs=1))
 
+        def bank(i, shape, dtype):
+            return psum.tile(shape, dtype, name="bank%d" % i, tag="bank%d" % i)
+
+        ident_bf = keep.tile([PARTS, PARTS], BF16, name="ident_bf")
+        make_identity(nc, ident_bf[:])
         ident = keep.tile([PARTS, PARTS], F32, name="ident")
         make_identity(nc, ident[:])
 
-        g_tiles = [keep.tile([PARTS, 1, PACK * SIDE * K], BF16, name="g_raw%d" % p) for p in range(SIDE)]
-        g_place = ((0, 0), (1, 0), (2, 0), (3, 0))
-        half_row = PACK * SIDE * K // 2
+        g_raw = keep.tile([PARTS, SIDE, PACK * SIDE * K], BF16, name="g_raw")
         for p in range(SIDE):
-            i, j = g_place[p]
-            cuts = (0, half_row, 2 * half_row) if p in SPLIT_LOADS else (0, 2 * half_row)
-            for a, b in zip(cuts[0:-1], cuts[1:]):
-                for h in range(2):
-                    nc.sync.dma_start(out=g_tiles[i][h:PARTS:2, j, a:b], in_=g_view[h, p][:, a:b])
-        g_views = [t[:].rearrange("p n (w q k) -> p n w q k", w=PACK, q=SIDE) for t in g_tiles]
+            for h in range(2):
+                nc.sync.dma_start(out=g_raw[h:PARTS:2, p, :], in_=g_view[h, p])
+        g_views = [g_raw[:, p].rearrange("p (w q k) -> p w q k", w=PACK, q=SIDE) for p in range(SIDE)]
         x_raw = keep.tile([PARTS, SIDE * SIDE, PACK * C], BF16, name="x_raw")
         for v in range(SIDE):
             nc.sync.dma_start(out=x_raw[:, SIDE * v : SIDE * (v + 1), :], in_=x_view[:, v])
@@ -77,9 +82,31 @@ def tile_iwht3layer_pa_s_kernel(tc, trans, weight, bias, grad_out, out):
         nc.vector.memset(gy_codes[:, 0:PAIR_COLS].bitcast(I32), 0)
         nc.vector.memset(gy_scales[:, 0:PAIR_COLS].bitcast(I32), 0)
 
-        gy_grouped = keep.tile([PARTS, PAIRS, 2, 2, K_PE, PACK], BF16, name="gy_grouped", align_bytes=64)
-        gy_by_place = gy_grouped[:].rearrange("p (v b) h a k w -> p b h a v k w", b=2)
+        gy_grouped = keep.tile([PARTS, PAIRS, 2, K, PACK], BF16, name="gy_grouped", align_bytes=64)
+        gy_by_place = gy_grouped[:].rearrange("p (v b) a k w -> p b a v k w", b=2)
         both = ((0, ADD), (1, SUB))
+
+        def butterfly(dst, src):
+            for bit, op in both:
+                nc.vector.tensor_tensor(out=dst[:, bit], in0=src[:, 0], in1=src[:, 1], op=op)
+
+        signs = [keep.tile([PARTS, PARTS], BF16, name="signs%d" % i) for i in range(4)]
+        from_rows = ident_bf[:].rearrange("p (a b w q x) -> p b a q x w", a=2, b=2, w=PACK, q=SIDE)
+        to_columns = signs[0][:].rearrange("p (q b a x w) -> p b a q x w", q=SIDE, b=2, a=2, x=2)
+        for p0 in range(2):
+            butterfly(to_columns[:, p0], from_rows[:, p0])
+        butterfly(
+            signs[1][:].rearrange("p (q b r) -> p b q r", q=SIDE, b=2),
+            signs[0][:].rearrange("p (q b r) -> p b q r", q=SIDE, b=2),
+        )
+        butterfly(
+            signs[2][:].rearrange("p (c r) -> p c r", c=2), signs[1][:].rearrange("p (c r) -> p c r", c=2)
+        )
+        butterfly(
+            signs[3][:].rearrange("p (c d r) -> p d c r", c=2, d=2),
+            signs[2][:].rearrange("p (c d r) -> p d c r", c=2, d=2),
+        )
+        hadamard = signs[3]
 
         g_f32 = [
             [keep.tile([PARTS, SIDE, PACK, SLOT], F32, name="g_f32_%d_%d" % (s, p)) for p in range(SIDE)]
@@ -92,10 +119,9 @@ def tile_iwht3layer_pa_s_kernel(tc, trans, weight, bias, grad_out, out):
         half_sums = [keep.tile([PARTS, SIDE, SLOT, PACK], F32, name="half_sum%d" % s) for s in range(SLOTS)]
 
         def cast(s, p):
-            i, j = g_place[p]
             nc.scalar.activation(
                 out=g_f32[s][p][:],
-                in_=g_views[i][:, j, :, :, SLOT * s : SLOT * (s + 1)].rearrange("p w q e -> p q w e"),
+                in_=g_views[p][:, :, :, SLOT * s : SLOT * (s + 1)].rearrange("p w q e -> p q w e"),
                 func=COPY,
                 scale=4.0,
             )
@@ -111,8 +137,8 @@ def tile_iwht3layer_pa_s_kernel(tc, trans, weight, bias, grad_out, out):
                     stop=(i == len(terms) - 1),
                 )
 
-        def new_banks():
-            return [psum.tile([PARTS, SIDE, PARTS], F32, name="bank", tag="bank") for g in range(SIDE)]
+        def new_banks(places):
+            return [bank(i, [PARTS, SIDE, PARTS], F32) for i in places]
 
         def turn_q(banks, s, p, g):
             add_up(banks[g][:, p, :], [g_f32[s][p][:, q].rearrange("p w e -> p (w e)") for q in PLUS[g]])
@@ -124,10 +150,9 @@ def tile_iwht3layer_pa_s_kernel(tc, trans, weight, bias, grad_out, out):
             for v in range(1, SIDE):
                 nc.vector.tensor_tensor(out=turned[s][v][:], in0=banks[v][:], in1=turned[s][0][:], op=SUB)
 
-        def turn_p(banks, s):
-            for g in range(SIDE):
-                for v in range(SIDE):
-                    add_up(banks[g][:, v, :], [turned[s][v][:, p, :] for p in PLUS[g]])
+        def turn_p(banks, s, g):
+            for v in range(SIDE):
+                add_up(banks[g][:, v, :], [turned[s][v][:, p, :] for p in PLUS[g]])
 
         def half_out_p(banks, s):
             nc.scalar.activation(
@@ -137,32 +162,73 @@ def tile_iwht3layer_pa_s_kernel(tc, trans, weight, bias, grad_out, out):
                 scale=0.5,
             )
             nc.scalar.copy(
-                out=gy_by_place[:, 0, 0, 0, :, SLOT * s : SLOT * (s + 1), :], in_=half_sums[s][:]
+                out=gy_by_place[:, 0, 0, :, SLOT * s : SLOT * (s + 1), :], in_=half_sums[s][:]
             )
 
         def rest_out_p(banks, s):
             for u in (2, 1, 3):
                 nc.vector.tensor_tensor(
-                    out=gy_by_place[:, u % 2, 0, u // 2, :, SLOT * s : SLOT * (s + 1), :],
+                    out=gy_by_place[:, u % 2, u // 2, :, SLOT * s : SLOT * (s + 1), :],
                     in0=banks[u][:].rearrange("p v (w e) -> p v e w", w=PACK),
                     in1=half_sums[s][:],
                     op=SUB,
                 )
 
+        mm_raw = keep.tile([PARTS, MM_STEPS, PIXELS, 2], BF16, name="mm_raw")
+        mm_turned = keep.tile([PARTS, MM_STEPS, PARTS], BF16, name="mm_turned")
+
+        def mm_collect():
+            nc.scalar.copy(
+                out=mm_raw[:],
+                in_=g_raw[:]
+                .rearrange("p s (j k) -> p (s j) k", k=K)[:, :, K_TOP:K]
+                .rearrange("p j (m x) -> p m j x", x=2),
+            )
+
+        def mm_turn(place):
+            flipped = bank(place, [PARTS, 2 * SIDE, PARTS], BF16)
+            for m in range(MM_STEPS):
+                nc.tensor.transpose(
+                    out=flipped[:, m, :], in_=mm_raw[:, m].rearrange("p j x -> p (j x)"), identity=ident_bf[:]
+                )
+            return flipped
+
+        def mm_turn_out(flipped):
+            nc.scalar.copy(out=mm_turned[:], in_=flipped[:, 0:MM_STEPS, :])
+
+        def mm_transform(place, part):
+            sums = bank(place, [PARTS, SIDE, PARTS], F32)
+            for i in range(MM_HALF):
+                nc.tensor.matmul(
+                    out=sums[:, i, :],
+                    lhsT=mm_turned[:, MM_HALF * part + i, :],
+                    rhs=hadamard[:],
+                    start=True,
+                    stop=True,
+                )
+            return sums
+
+        def mm_out(sums, part):
+            first = PACK * (K_TOP + 2 * MM_HALF * part)
+            nc.scalar.copy(
+                out=gy_grouped[:]
+                .rearrange("p n a k w -> p (n a) (k w)")[:, :, first : first + 2 * PACK * MM_HALF]
+                .rearrange("p j (m y) -> p j m y", y=2 * PACK),
+                in_=sums[:, 0:MM_HALF, :].rearrange("p m (j y) -> p j m y", y=2 * PACK),
+            )
+
         half_q = [keep.tile([PARTS, SIDE, PACK, 2, K_VE], F32, name="half_q%d" % a) for a in range(2)]
         done_q = [keep.tile([PARTS, 2, SIDE, PACK, K_VE], F32, name="done_q%d" % a) for a in range(2)]
-        half_p = [keep.tile([PARTS, 2, 2, PACK, 2, K_VE], F32, name="half_p%d" % a) for a in range(2)]
+        half_p = [keep.tile([PARTS, 2, 2, PACK, 2, K_ROW], F32, name="half_p%d" % a) for a in range(2)]
 
         def step_q1(p):
-            cuts = (0, PACK // 2, PACK) if p in SPLIT_LOADS else (0, PACK)
-            for a, b in zip(cuts[0:-1], cuts[1:]):
-                for v1, op in both:
-                    nc.vector.tensor_tensor(
-                        out=half_q[v1][:, p, a:b],
-                        in0=g_views[p][:, 0, a:b, 0:2, K_PE:K],
-                        in1=g_views[p][:, 0, a:b, 2:4, K_PE:K],
-                        op=op,
-                    )
+            for v1, op in both:
+                nc.vector.tensor_tensor(
+                    out=half_q[v1][:, p],
+                    in0=g_views[p][:, :, 0:2, K_PE:K_TOP],
+                    in1=g_views[p][:, :, 2:4, K_PE:K_TOP],
+                    op=op,
+                )
 
         def step_q0(v1):
             for v0, op in both:
@@ -177,19 +243,20 @@ def tile_iwht3layer_pa_s_kernel(tc, trans, weight, bias, grad_out, out):
             src = done_q[v1][:].rearrange("p v (a b) w k -> p a v (b w) k", a=2)
             dst = half_p[v1][:].rearrange("p v b w a k -> p a v (b w) k")
             engine.tensor_tensor(
-                out=dst[:, u1, some], in0=src[:, 0, some], in1=src[:, 1, some], op=both[u1][1]
+                out=dst[:, u1, some, :, 0:K_VE], in0=src[:, 0, some], in1=src[:, 1, some], op=both[u1][1]
             )
 
         def step_p0_one(v, u0, on_gpsimd=False):
-            src = half_p[v // 2][:, v % 2]
-            dst = gy_grouped[:, 2 * v + u0, 1]
+            src = half_p[v // 2][:, v % 2, :, :, :, 0:K_VE]
+            dst = gy_grouped[:, 2 * v + u0, :, K_PE:K_TOP, :]
             if not on_gpsimd:
-                nc.vector.tensor_tensor(
-                    out=dst.rearrange("p a (r e) w -> p (a r) w e", e=RUN),
-                    in0=src[:, 0].rearrange("p w a (r e) -> p (a r) w e", e=RUN),
-                    in1=src[:, 1].rearrange("p w a (r e) -> p (a r) w e", e=RUN),
-                    op=both[u0][1],
-                )
+                for u1 in range(2):
+                    nc.vector.tensor_tensor(
+                        out=dst[:, u1].rearrange("p (r e) w -> p r w e", e=RUN),
+                        in0=src[:, 0, :, u1, :].rearrange("p w (r e) -> p r w e", e=RUN),
+                        in1=src[:, 1, :, u1, :].rearrange("p w (r e) -> p r w e", e=RUN),
+                        op=both[u0][1],
+                    )
             else:
                 nc.gpsimd.tensor_tensor(
                     out=dst,
@@ -202,8 +269,9 @@ def tile_iwht3layer_pa_s_kernel(tc, trans, weight, bias, grad_out, out):
         x_codes = keep.tile([PARTS, SIDE * SIDE, C], U32, name="x_codes", align_bytes=64)
         x_scales = keep.tile([PARTS, SIDE * SIDE, C], U8, name="x_scales", align_bytes=64)
 
-        def regroup(v):
-            for t in range(SIDE * v, SIDE * (v + 1)):
+        def regroup(v, some=(0, 1, 2, 3)):
+            for u in some:
+                t = SIDE * v + u
                 nc.scalar.copy(
                     out=x_grouped[:, t].rearrange("p (r e) w -> p r w e", e=RUN),
                     in_=x_raw[:, t].rearrange("p (w r e) -> p r w e", w=PACK, e=RUN),
@@ -224,12 +292,12 @@ def tile_iwht3layer_pa_s_kernel(tc, trans, weight, bias, grad_out, out):
             nc.vector.quantize_mx(
                 out=gy_codes[:, fresh].bitcast(E5M2_X4),
                 scales=gy_scales[:, fresh],
-                in_=gy_grouped[:, pair].rearrange("p h a k w -> p (h a k w)"),
+                in_=gy_grouped[:, pair].rearrange("p a k w -> p (a k w)"),
             )
             window = slice(pair * PAIR_COLS, pair * PAIR_COLS + N_PASS)
             result = outs.tile([PARTS, 2, K], F32, name="result", tag="result")
             for u1 in range(2):
-                acc = psum.tile([PARTS, N_PASS], F32, name="acc", tag="bank")
+                acc = bank((2 * pair + u1) % 8, [PARTS, N_PASS], F32)
                 t = SIDE * v + 2 * u1 + u0
                 nc.tensor.matmul_mx(
                     out=acc[:],
@@ -241,22 +309,26 @@ def tile_iwht3layer_pa_s_kernel(tc, trans, weight, bias, grad_out, out):
                     stop=True,
                 )
                 nc.scalar.activation(
-                    out=result[:, u1, :].rearrange("p (h k) -> p h k", h=2),
-                    in_=acc[:, N_PASS - PAIR_COLS : N_PASS].rearrange("p (h a k) -> p a h k", h=2, a=2)[:, u1],
+                    out=result[:, u1, :],
+                    in_=acc[:, N_PASS - PAIR_COLS + K * u1 : N_PASS - PAIR_COLS + K * (u1 + 1)],
                     func=COPY,
                     scale=1.0 / (SIDE * SIDE),
                 )
             nc.sync.dma_start(out=out_view[:, v, u0], in_=result[:])
 
-        banks_q0 = new_banks()
+        banks_q0 = new_banks((0, 1, 2, 3))
         for p in range(SIDE):
             cast(0, p)
-            cast(1, p)
+            if p < 2:
+                cast(1, p)
             step_q1(p)
             for g in range(SIDE):
                 turn_q(banks_q0, 0, p, g)
+        cast(1, 2)
+        cast(1, 3)
         half_out_q(banks_q0, 0)
-        banks_q1 = new_banks()
+        mm_collect()
+        banks_q1 = new_banks((4, 5, 6, 7))
         for g in range(SIDE):
             for p in range(SIDE):
                 turn_q(banks_q1, 1, p, g)
@@ -266,42 +338,58 @@ def tile_iwht3layer_pa_s_kernel(tc, trans, weight, bias, grad_out, out):
         step_q0(0)
         step_p1(nc.gpsimd, 0, 0, high)
         rest_out_q(banks_q0, 0)
-        banks_p0 = new_banks()
-        turn_p(banks_p0, 0)
         half_out_q(banks_q1, 1)
+        flipped = mm_turn(0)
+        banks_p0 = new_banks((1, 2, 3, 4))
+        for g in range(SIDE):
+            turn_p(banks_p0, 0, g)
         regroup(0)
+        mm_turn_out(flipped)
         regroup(1)
         step_p1(nc.vector, 0, 0, low)
         step_p1(nc.vector, 0, 1, whole)
         step_p0_one(1, 1, True)
         rest_out_q(banks_q1, 1)
-        banks_p1 = new_banks()
-        turn_p(banks_p1, 1)
+        banks_p1 = new_banks((5, 6, 7, 0))
+        turn_p(banks_p1, 1, 0)
+        turn_p(banks_p1, 1, 1)
         half_out_p(banks_p0, 0)
+        sums0 = mm_transform(1, 0)
+        turn_p(banks_p1, 1, 2)
         half_out_p(banks_p1, 1)
-        regroup(2)
-        regroup(3)
+        sums1 = mm_transform(5, 1)
+        turn_p(banks_p1, 1, 3)
+        regroup(2, (0,))
+        mm_out(sums0, 0)
+        mm_out(sums1, 1)
+        regroup(2, (1, 2, 3))
         step_p0_one(0, 0)
         step_p0_one(0, 1)
         step_p0_one(1, 0)
-        quantise_x(0, 2)
+        quantise_x(0, 1)
         step_q0(1)
         step_p1(nc.gpsimd, 1, 0, high)
         step_p1(nc.gpsimd, 1, 1, high)
         rest_out_p(banks_p0, 0)
         rest_out_p(banks_p1, 1)
         finish(0, 0)
+        regroup(3, (0,))
         step_p1(nc.vector, 1, 0, low)
         finish(0, 1)
+        regroup(3, (1,))
         step_p1(nc.vector, 1, 1, low)
+        quantise_x(1, 1)
         finish(1, 0)
-        quantise_x(2, 2)
-        finish(1, 1)
+        regroup(3, (2,))
         step_p0_one(2, 0)
+        finish(1, 1)
+        regroup(3, (3,))
         step_p0_one(2, 1)
+        quantise_x(2, 1)
         finish(2, 0)
         step_p0_one(3, 0)
         finish(2, 1)
         step_p0_one(3, 1)
+        quantise_x(3, 1)
         finish(3, 0)
         finish(3, 1)

@@ -25,12 +25,11 @@ K = 128
 RUN = 4
 N_PASS = 512
 PAD_BLOCKS = N_PASS // K - 1
-SLOT = PARTS // PACK
 SLOTS = 2
-K_PE = SLOT * SLOTS
+PART_W = PACK // SLOTS
+K_PE = PARTS // PART_W
 K_MM = 12
 MM_STEPS = K_MM // 2
-MM_HALF = MM_STEPS // 2
 K_VE = K - K_PE - K_MM
 K_TOP = K_PE + K_VE
 K_ROW = 56
@@ -38,6 +37,9 @@ PIXELS = SIDE * PACK * SIDE
 PLUS = ((0, 1, 2, 3), (0, 2), (0, 1), (0, 3))
 PAIRS = 8
 PAIR_COLS = 2 * K
+FIRST_BANKS = (1, 4, 5, 0)
+LAST_BANKS = (2, 3, 6, 7)
+PASS_BANKS = FIRST_BANKS + FIRST_BANKS + LAST_BANKS + FIRST_BANKS
 
 
 def tile_iwht3layer_pa_s_kernel(tc, trans, weight, bias, grad_out, out):
@@ -109,19 +111,19 @@ def tile_iwht3layer_pa_s_kernel(tc, trans, weight, bias, grad_out, out):
         hadamard = signs[3]
 
         g_f32 = [
-            [keep.tile([PARTS, SIDE, PACK, SLOT], F32, name="g_f32_%d_%d" % (s, p)) for p in range(SIDE)]
+            [keep.tile([PARTS, SIDE, PART_W, K_PE], F32, name="g_f32_%d_%d" % (s, p)) for p in range(SIDE)]
             for s in range(SLOTS)
         ]
         turned = [
             [keep.tile([PARTS, SIDE, PARTS], F32, name="turned%d_%d" % (s, v)) for v in range(SIDE)]
             for s in range(SLOTS)
         ]
-        half_sums = [keep.tile([PARTS, SIDE, SLOT, PACK], F32, name="half_sum%d" % s) for s in range(SLOTS)]
+        half_sums = [keep.tile([PARTS, 2, K_PE, PACK], F32, name="half_sum%d" % c) for c in range(2)]
 
         def cast(s, p):
             nc.scalar.activation(
                 out=g_f32[s][p][:],
-                in_=g_views[p][:, :, :, SLOT * s : SLOT * (s + 1)].rearrange("p w q e -> p q w e"),
+                in_=g_views[p][:, PART_W * s : PART_W * (s + 1), :, 0:K_PE].rearrange("p w q k -> p q w k"),
                 func=COPY,
                 scale=4.0,
             )
@@ -141,7 +143,7 @@ def tile_iwht3layer_pa_s_kernel(tc, trans, weight, bias, grad_out, out):
             return [bank(i, [PARTS, SIDE, PARTS], F32) for i in places]
 
         def turn_q(banks, s, p, g):
-            add_up(banks[g][:, p, :], [g_f32[s][p][:, q].rearrange("p w e -> p (w e)") for q in PLUS[g]])
+            add_up(banks[g][:, p, :], [g_f32[s][p][:, q].rearrange("p w k -> p (w k)") for q in PLUS[g]])
 
         def half_out_q(banks, s):
             nc.scalar.activation(out=turned[s][0][:], in_=banks[0][:], func=COPY, scale=0.5)
@@ -150,27 +152,24 @@ def tile_iwht3layer_pa_s_kernel(tc, trans, weight, bias, grad_out, out):
             for v in range(1, SIDE):
                 nc.vector.tensor_tensor(out=turned[s][v][:], in0=banks[v][:], in1=turned[s][0][:], op=SUB)
 
-        def turn_p(banks, s, g):
-            for v in range(SIDE):
-                add_up(banks[g][:, v, :], [turned[s][v][:, p, :] for p in PLUS[g]])
+        def turn_p(banks, v1, g):
+            for v0 in range(2):
+                for s in range(SLOTS):
+                    add_up(banks[g][:, SLOTS * v0 + s, :], [turned[s][2 * v1 + v0][:, p, :] for p in PLUS[g]])
 
-        def half_out_p(banks, s):
-            nc.scalar.activation(
-                out=half_sums[s][:],
-                in_=banks[0][:].rearrange("p v (w e) -> p v e w", w=PACK),
-                func=COPY,
-                scale=0.5,
-            )
-            nc.scalar.copy(
-                out=gy_by_place[:, 0, 0, :, SLOT * s : SLOT * (s + 1), :], in_=half_sums[s][:]
-            )
+        def by_channel(one_bank):
+            return one_bank[:].rearrange("p r c -> p (r c)").rearrange("p (d w k) -> p d k w", d=2, w=PACK)
 
-        def rest_out_p(banks, s):
+        def half_out_p(banks, v1):
+            nc.scalar.activation(out=half_sums[v1][:], in_=by_channel(banks[0]), func=COPY, scale=0.5)
+            nc.scalar.copy(out=gy_by_place[:, 0, 0, 2 * v1 : 2 * v1 + 2, 0:K_PE, :], in_=half_sums[v1][:])
+
+        def rest_out_p(banks, v1):
             for u in (2, 1, 3):
                 nc.vector.tensor_tensor(
-                    out=gy_by_place[:, u % 2, u // 2, :, SLOT * s : SLOT * (s + 1), :],
-                    in0=banks[u][:].rearrange("p v (w e) -> p v e w", w=PACK),
-                    in1=half_sums[s][:],
+                    out=gy_by_place[:, u % 2, u // 2, 2 * v1 : 2 * v1 + 2, 0:K_PE, :],
+                    in0=by_channel(banks[u]),
+                    in1=half_sums[v1][:],
                     op=SUB,
                 )
 
@@ -196,25 +195,19 @@ def tile_iwht3layer_pa_s_kernel(tc, trans, weight, bias, grad_out, out):
         def mm_turn_out(flipped):
             nc.scalar.copy(out=mm_turned[:], in_=flipped[:, 0:MM_STEPS, :])
 
-        def mm_transform(place, part):
-            sums = bank(place, [PARTS, SIDE, PARTS], F32)
-            for i in range(MM_HALF):
-                nc.tensor.matmul(
-                    out=sums[:, i, :],
-                    lhsT=mm_turned[:, MM_HALF * part + i, :],
-                    rhs=hadamard[:],
-                    start=True,
-                    stop=True,
-                )
+        def mm_transform(place):
+            sums = bank(place, [PARTS, 2 * SIDE, PARTS], BF16)
+            for m in range(MM_STEPS):
+                nc.tensor.matmul(out=sums[:, m, :], lhsT=mm_turned[:, m, :], rhs=hadamard[:], start=True, stop=True)
             return sums
 
-        def mm_out(sums, part):
-            first = PACK * (K_TOP + 2 * MM_HALF * part)
+        def mm_out(sums):
+            first = PACK * K_TOP
             nc.scalar.copy(
                 out=gy_grouped[:]
-                .rearrange("p n a k w -> p (n a) (k w)")[:, :, first : first + 2 * PACK * MM_HALF]
+                .rearrange("p n a k w -> p (n a) (k w)")[:, :, first : first + 2 * PACK * MM_STEPS]
                 .rearrange("p j (m y) -> p j m y", y=2 * PACK),
-                in_=sums[:, 0:MM_HALF, :].rearrange("p m (j y) -> p j m y", y=2 * PACK),
+                in_=sums[:, 0:MM_STEPS, :].rearrange("p m (j y) -> p j m y", y=2 * PACK),
             )
 
         half_q = [keep.tile([PARTS, SIDE, PACK, 2, K_VE], F32, name="half_q%d" % a) for a in range(2)]
@@ -230,8 +223,8 @@ def tile_iwht3layer_pa_s_kernel(tc, trans, weight, bias, grad_out, out):
                     op=op,
                 )
 
-        def step_q0(v1):
-            for v0, op in both:
+        def step_q0(v1, some=both):
+            for v0, op in some:
                 nc.vector.tensor_tensor(
                     out=done_q[v1][:, v0],
                     in0=half_q[v1][:, :, :, 0, :],
@@ -297,7 +290,7 @@ def tile_iwht3layer_pa_s_kernel(tc, trans, weight, bias, grad_out, out):
             window = slice(pair * PAIR_COLS, pair * PAIR_COLS + N_PASS)
             result = outs.tile([PARTS, 2, K], F32, name="result", tag="result")
             for u1 in range(2):
-                acc = bank((2 * pair + u1) % 8, [PARTS, N_PASS], F32)
+                acc = bank(PASS_BANKS[2 * pair + u1], [PARTS, N_PASS], F32)
                 t = SIDE * v + 2 * u1 + u0
                 nc.tensor.matmul_mx(
                     out=acc[:],
@@ -334,56 +327,55 @@ def tile_iwht3layer_pa_s_kernel(tc, trans, weight, bias, grad_out, out):
                 turn_q(banks_q1, 1, p, g)
         low = slice(0, 1)
         high = slice(1, 2)
-        whole = slice(0, 2)
         step_q0(0)
         step_p1(nc.gpsimd, 0, 0, high)
+        step_p1(nc.gpsimd, 0, 1, high)
         rest_out_q(banks_q0, 0)
         half_out_q(banks_q1, 1)
+        rest_out_q(banks_q1, 1)
         flipped = mm_turn(0)
-        banks_p0 = new_banks((1, 2, 3, 4))
-        for g in range(SIDE):
-            turn_p(banks_p0, 0, g)
+        banks_first = new_banks(FIRST_BANKS[0:3])
+        turn_p(banks_first, 0, 0)
         regroup(0)
         mm_turn_out(flipped)
+        sums = mm_transform(0)
+        turn_p(banks_first, 0, 1)
+        turn_p(banks_first, 0, 2)
+        half_out_p(banks_first, 0)
+        mm_out(sums)
+        banks_first.extend(new_banks(FIRST_BANKS[3:4]))
+        turn_p(banks_first, 0, 3)
+        banks_last = new_banks(LAST_BANKS)
+        for g in range(SIDE):
+            turn_p(banks_last, 1, g)
         regroup(1)
+        half_out_p(banks_last, 1)
+        regroup(2)
         step_p1(nc.vector, 0, 0, low)
-        step_p1(nc.vector, 0, 1, whole)
-        step_p0_one(1, 1, True)
-        rest_out_q(banks_q1, 1)
-        banks_p1 = new_banks((5, 6, 7, 0))
-        turn_p(banks_p1, 1, 0)
-        turn_p(banks_p1, 1, 1)
-        half_out_p(banks_p0, 0)
-        sums0 = mm_transform(1, 0)
-        turn_p(banks_p1, 1, 2)
-        half_out_p(banks_p1, 1)
-        sums1 = mm_transform(5, 1)
-        turn_p(banks_p1, 1, 3)
-        regroup(2, (0,))
-        mm_out(sums0, 0)
-        mm_out(sums1, 1)
-        regroup(2, (1, 2, 3))
+        step_p1(nc.vector, 0, 1, low)
         step_p0_one(0, 0)
         step_p0_one(0, 1)
         step_p0_one(1, 0)
+        step_p0_one(1, 1)
         quantise_x(0, 1)
-        step_q0(1)
-        step_p1(nc.gpsimd, 1, 0, high)
-        step_p1(nc.gpsimd, 1, 1, high)
-        rest_out_p(banks_p0, 0)
-        rest_out_p(banks_p1, 1)
+        step_q0(1, both[0:1])
+        step_p1(nc.gpsimd, 1, 0, low)
+        rest_out_p(banks_first, 0)
         finish(0, 0)
         regroup(3, (0,))
-        step_p1(nc.vector, 1, 0, low)
+        step_p1(nc.vector, 1, 1, low)
         finish(0, 1)
         regroup(3, (1,))
-        step_p1(nc.vector, 1, 1, low)
         quantise_x(1, 1)
         finish(1, 0)
         regroup(3, (2,))
-        step_p0_one(2, 0)
+        step_q0(1, both[1:2])
+        step_p1(nc.gpsimd, 1, 0, high)
+        rest_out_p(banks_last, 1)
         finish(1, 1)
         regroup(3, (3,))
+        step_p1(nc.vector, 1, 1, high)
+        step_p0_one(2, 0)
         step_p0_one(2, 1)
         quantise_x(2, 1)
         finish(2, 0)

@@ -223,12 +223,12 @@ def tile_iwht3layer_pa_s_kernel(tc, trans, weight, bias, grad_out, out):
                     op=op,
                 )
 
-        def step_q0(v1, some=both):
+        def step_q0(v1, some=both, rows=slice(0, SIDE)):
             for v0, op in some:
                 nc.vector.tensor_tensor(
-                    out=done_q[v1][:, v0],
-                    in0=half_q[v1][:, :, :, 0, :],
-                    in1=half_q[v1][:, :, :, 1, :],
+                    out=done_q[v1][:, v0, rows],
+                    in0=half_q[v1][:, rows, :, 0, :],
+                    in1=half_q[v1][:, rows, :, 1, :],
                     op=op,
                 )
 
@@ -312,12 +312,13 @@ def tile_iwht3layer_pa_s_kernel(tc, trans, weight, bias, grad_out, out):
         banks_q0 = new_banks((0, 1, 2, 3))
         for p in range(SIDE):
             cast(0, p)
-            if p < 2:
+            if p < 3:
                 cast(1, p)
             step_q1(p)
+            if p == 1:
+                step_q0(0, both, slice(0, 2))
             for g in range(SIDE):
                 turn_q(banks_q0, 0, p, g)
-        cast(1, 2)
         cast(1, 3)
         half_out_q(banks_q0, 0)
         mm_collect()
@@ -327,7 +328,10 @@ def tile_iwht3layer_pa_s_kernel(tc, trans, weight, bias, grad_out, out):
                 turn_q(banks_q1, 1, p, g)
         low = slice(0, 1)
         high = slice(1, 2)
-        step_q0(0)
+        step_q0(0, both[0:1], slice(2, SIDE))
+        step_p1(nc.vector, 0, 0, low)
+        step_p1(nc.vector, 0, 1, low)
+        step_q0(0, both[1:2], slice(2, SIDE))
         step_p1(nc.gpsimd, 0, 0, high)
         step_p1(nc.gpsimd, 0, 1, high)
         rest_out_q(banks_q0, 0)
@@ -349,10 +353,9 @@ def tile_iwht3layer_pa_s_kernel(tc, trans, weight, bias, grad_out, out):
         for g in range(SIDE):
             turn_p(banks_last, 1, g)
         regroup(1)
+        regroup(2, (0, 1))
         half_out_p(banks_last, 1)
-        regroup(2)
-        step_p1(nc.vector, 0, 0, low)
-        step_p1(nc.vector, 0, 1, low)
+        regroup(2, (2, 3))
         step_p0_one(0, 0)
         step_p0_one(0, 1)
         step_p0_one(1, 0)
@@ -381,7 +384,7 @@ def tile_iwht3layer_pa_s_kernel(tc, trans, weight, bias, grad_out, out):
         finish(2, 0)
         step_p0_one(3, 0)
         finish(2, 1)
-        step_p0_one(3, 1)
         quantise_x(3, 1)
         finish(3, 0)
+        step_p0_one(3, 1)
         finish(3, 1)

@@ -279,35 +279,55 @@ def tile_iwht3layer_pa_s_kernel(tc, trans, weight, bias, grad_out, out):
                 in_=x_grouped[:, start:stop].rearrange("p t c w -> p (t c w)"),
             )
 
-        def finish(v, u0):
+        def finish(v, u0, one_by_one=False):
             pair = 2 * v + u0
-            fresh = slice((1 + pair) * PAIR_COLS, (2 + pair) * PAIR_COLS)
-            nc.vector.quantize_mx(
-                out=gy_codes[:, fresh].bitcast(E5M2_X4),
-                scales=gy_scales[:, fresh],
-                in_=gy_grouped[:, pair].rearrange("p a k w -> p (a k w)"),
-            )
-            window = slice(pair * PAIR_COLS, pair * PAIR_COLS + N_PASS)
+            first = (1 + pair) * PAIR_COLS
+            if not one_by_one:
+                nc.vector.quantize_mx(
+                    out=gy_codes[:, first : first + PAIR_COLS].bitcast(E5M2_X4),
+                    scales=gy_scales[:, first : first + PAIR_COLS],
+                    in_=gy_grouped[:, pair].rearrange("p a k w -> p (a k w)"),
+                )
             result = outs.tile([PARTS, 2, K], F32, name="result", tag="result")
             for u1 in range(2):
+                if one_by_one:
+                    nc.vector.quantize_mx(
+                        out=gy_codes[:, first + K * u1 : first + K * (u1 + 1)].bitcast(E5M2_X4),
+                        scales=gy_scales[:, first + K * u1 : first + K * (u1 + 1)],
+                        in_=gy_grouped[:, pair, u1].rearrange("p k w -> p (k w)"),
+                    )
+                stop = first + (K * (u1 + 1) if one_by_one else PAIR_COLS)
+                wanted = N_PASS - (stop - first) + K * u1
                 acc = bank(PASS_BANKS[2 * pair + u1], [PARTS, N_PASS], F32)
                 t = SIDE * v + 2 * u1 + u0
                 nc.tensor.matmul_mx(
                     out=acc[:],
                     lhsT=x_codes[:, t, :].bitcast(E4M3_X4),
                     lhsT_scale=x_scales[:, t, :],
-                    rhs=gy_codes[:, window].bitcast(E5M2_X4),
-                    rhs_scale=gy_scales[:, window],
+                    rhs=gy_codes[:, stop - N_PASS : stop].bitcast(E5M2_X4),
+                    rhs_scale=gy_scales[:, stop - N_PASS : stop],
                     start=True,
                     stop=True,
                 )
                 nc.scalar.activation(
-                    out=result[:, u1, :],
-                    in_=acc[:, N_PASS - PAIR_COLS + K * u1 : N_PASS - PAIR_COLS + K * (u1 + 1)],
-                    func=COPY,
-                    scale=1.0 / (SIDE * SIDE),
+                    out=result[:, u1, :], in_=acc[:, wanted : wanted + K], func=COPY, scale=1.0 / (SIDE * SIDE)
                 )
             nc.sync.dma_start(out=out_view[:, v, u0], in_=result[:])
+
+        def keep_clock(v, u0, places):
+            stop = (2 + 2 * v + u0) * PAIR_COLS
+            for u1, place in enumerate(places):
+                spare = bank(place, [PARTS, N_PASS], F32)
+                t = SIDE * v + 2 * u1 + u0
+                nc.tensor.matmul_mx(
+                    out=spare[:],
+                    lhsT=x_codes[:, t, :].bitcast(E4M3_X4),
+                    lhsT_scale=x_scales[:, t, :],
+                    rhs=gy_codes[:, stop - N_PASS : stop].bitcast(E5M2_X4),
+                    rhs_scale=gy_scales[:, stop - N_PASS : stop],
+                    start=True,
+                    stop=True,
+                )
 
         banks_q0 = new_banks((0, 1, 2, 3))
         for p in range(SIDE):
@@ -316,10 +336,11 @@ def tile_iwht3layer_pa_s_kernel(tc, trans, weight, bias, grad_out, out):
                 cast(1, p)
             step_q1(p)
             if p == 1:
-                step_q0(0, both, slice(0, 2))
+                step_q0(0, both[0:1], slice(0, 2))
             for g in range(SIDE):
                 turn_q(banks_q0, 0, p, g)
         cast(1, 3)
+        regroup(0, (0,))
         half_out_q(banks_q0, 0)
         mm_collect()
         banks_q1 = new_banks((4, 5, 6, 7))
@@ -329,6 +350,7 @@ def tile_iwht3layer_pa_s_kernel(tc, trans, weight, bias, grad_out, out):
         low = slice(0, 1)
         high = slice(1, 2)
         step_q0(0, both[0:1], slice(2, SIDE))
+        step_q0(0, both[1:2], slice(0, 2))
         step_p1(nc.vector, 0, 0, low)
         step_p1(nc.vector, 0, 1, low)
         step_q0(0, both[1:2], slice(2, SIDE))
@@ -340,22 +362,22 @@ def tile_iwht3layer_pa_s_kernel(tc, trans, weight, bias, grad_out, out):
         flipped = mm_turn(0)
         banks_first = new_banks(FIRST_BANKS[0:3])
         turn_p(banks_first, 0, 0)
-        regroup(0)
+        regroup(0, (1, 2, 3))
         mm_turn_out(flipped)
         sums = mm_transform(0)
         turn_p(banks_first, 0, 1)
         turn_p(banks_first, 0, 2)
-        half_out_p(banks_first, 0)
+        regroup(1, (0,))
         mm_out(sums)
         banks_first.extend(new_banks(FIRST_BANKS[3:4]))
         turn_p(banks_first, 0, 3)
+        half_out_p(banks_first, 0)
         banks_last = new_banks(LAST_BANKS)
         for g in range(SIDE):
             turn_p(banks_last, 1, g)
-        regroup(1)
+        regroup(1, (1, 2, 3))
         regroup(2, (0, 1))
         half_out_p(banks_last, 1)
-        regroup(2, (2, 3))
         step_p0_one(0, 0)
         step_p0_one(0, 1)
         step_p0_one(1, 0)
@@ -365,18 +387,20 @@ def tile_iwht3layer_pa_s_kernel(tc, trans, weight, bias, grad_out, out):
         step_p1(nc.gpsimd, 1, 0, low)
         rest_out_p(banks_first, 0)
         finish(0, 0)
-        regroup(3, (0,))
+        regroup(2, (2,))
         step_p1(nc.vector, 1, 1, low)
         finish(0, 1)
-        regroup(3, (1,))
+        regroup(2, (3,))
         quantise_x(1, 1)
         finish(1, 0)
-        regroup(3, (2,))
+        keep_clock(1, 0, PASS_BANKS[6:8])
+        regroup(3, (0, 1))
         step_q0(1, both[1:2])
         step_p1(nc.gpsimd, 1, 0, high)
         rest_out_p(banks_last, 1)
         finish(1, 1)
-        regroup(3, (3,))
+        keep_clock(1, 1, PASS_BANKS[8:10])
+        regroup(3, (2, 3))
         step_p1(nc.vector, 1, 1, high)
         step_p0_one(2, 0)
         step_p0_one(2, 1)
@@ -387,4 +411,4 @@ def tile_iwht3layer_pa_s_kernel(tc, trans, weight, bias, grad_out, out):
         quantise_x(3, 1)
         finish(3, 0)
         step_p0_one(3, 1)
-        finish(3, 1)
+        finish(3, 1, True)

@@ -66,7 +66,12 @@ def tile_iwht3layer_pa_s_kernel(tc, trans, weight, bias, grad_out, out):
         make_identity(nc, ident[:])
 
         g_raw = keep.tile([PARTS, SIDE, PACK * SIDE * K], BF16, name="g_raw")
-        for p in range(SIDE):
+        part_cols = PART_W * SIDE * K
+        for s in range(SLOTS):
+            for h in range(2):
+                cols = slice(part_cols * s, part_cols * (s + 1))
+                nc.sync.dma_start(out=g_raw[h:PARTS:2, 0, cols], in_=g_view[h, 0][:, cols])
+        for p in range(1, SIDE):
             for h in range(2):
                 nc.sync.dma_start(out=g_raw[h:PARTS:2, p, :], in_=g_view[h, p])
         g_views = [g_raw[:, p].rearrange("p (w q k) -> p w q k", w=PACK, q=SIDE) for p in range(SIDE)]
@@ -214,12 +219,12 @@ def tile_iwht3layer_pa_s_kernel(tc, trans, weight, bias, grad_out, out):
         done_q = [keep.tile([PARTS, 2, SIDE, PACK, K_VE], F32, name="done_q%d" % a) for a in range(2)]
         half_p = [keep.tile([PARTS, 2, 2, PACK, 2, K_ROW], F32, name="half_p%d" % a) for a in range(2)]
 
-        def step_q1(p):
+        def step_q1(p, some=slice(0, PACK)):
             for v1, op in both:
                 nc.vector.tensor_tensor(
-                    out=half_q[v1][:, p],
-                    in0=g_views[p][:, :, 0:2, K_PE:K_TOP],
-                    in1=g_views[p][:, :, 2:4, K_PE:K_TOP],
+                    out=half_q[v1][:, p, some],
+                    in0=g_views[p][:, some, 0:2, K_PE:K_TOP],
+                    in1=g_views[p][:, some, 2:4, K_PE:K_TOP],
                     op=op,
                 )
 
@@ -312,7 +317,10 @@ def tile_iwht3layer_pa_s_kernel(tc, trans, weight, bias, grad_out, out):
                 nc.scalar.activation(
                     out=result[:, u1, :], in_=acc[:, wanted : wanted + K], func=COPY, scale=1.0 / (SIDE * SIDE)
                 )
-            nc.sync.dma_start(out=out_view[:, v, u0], in_=result[:])
+                if one_by_one:
+                    nc.sync.dma_start(out=out_view[:, v, u0, u1], in_=result[:, u1, :])
+            if not one_by_one:
+                nc.sync.dma_start(out=out_view[:, v, u0], in_=result[:])
 
         def keep_clock(v, u0, places):
             stop = (2 + 2 * v + u0) * PAIR_COLS
@@ -334,9 +342,13 @@ def tile_iwht3layer_pa_s_kernel(tc, trans, weight, bias, grad_out, out):
             cast(0, p)
             if p < 3:
                 cast(1, p)
-            step_q1(p)
-            if p == 1:
-                step_q0(0, both[0:1], slice(0, 2))
+            if p == 0:
+                step_q1(p, slice(0, PART_W))
+                step_q1(p, slice(PART_W, PACK))
+            else:
+                step_q1(p)
+            if p < 2:
+                step_q0(0, both, slice(p, p + 1))
             for g in range(SIDE):
                 turn_q(banks_q0, 0, p, g)
         cast(1, 3)
@@ -350,10 +362,10 @@ def tile_iwht3layer_pa_s_kernel(tc, trans, weight, bias, grad_out, out):
         low = slice(0, 1)
         high = slice(1, 2)
         step_q0(0, both[0:1], slice(2, SIDE))
-        step_q0(0, both[1:2], slice(0, 2))
+        step_q0(0, both[1:2], slice(2, 3))
         step_p1(nc.vector, 0, 0, low)
         step_p1(nc.vector, 0, 1, low)
-        step_q0(0, both[1:2], slice(2, SIDE))
+        step_q0(0, both[1:2], slice(3, SIDE))
         step_p1(nc.gpsimd, 0, 0, high)
         step_p1(nc.gpsimd, 0, 1, high)
         rest_out_q(banks_q0, 0)

@@ -228,9 +228,9 @@ def tile_iwht3layer_pa_s_kernel(tc, trans, weight, bias, grad_out, out):
                     op=op,
                 )
 
-        def step_q0(v1, some=both, rows=slice(0, SIDE)):
+        def step_q0(v1, some=both, rows=slice(0, SIDE), engine=nc.vector):
             for v0, op in some:
-                nc.vector.tensor_tensor(
+                engine.tensor_tensor(
                     out=done_q[v1][:, v0, rows],
                     in0=half_q[v1][:, rows, :, 0, :],
                     in1=half_q[v1][:, rows, :, 1, :],
@@ -364,10 +364,11 @@ def tile_iwht3layer_pa_s_kernel(tc, trans, weight, bias, grad_out, out):
         step_q0(0, both[0:1], slice(2, SIDE))
         step_q0(0, both[1:2], slice(2, 3))
         step_p1(nc.vector, 0, 0, low)
-        step_p1(nc.vector, 0, 1, low)
         step_q0(0, both[1:2], slice(3, SIDE))
+        step_p1(nc.vector, 0, 1, low)
         step_p1(nc.gpsimd, 0, 0, high)
         step_p1(nc.gpsimd, 0, 1, high)
+        step_q0(1, both[0:1], slice(0, 1), nc.gpsimd)
         rest_out_q(banks_q0, 0)
         half_out_q(banks_q1, 1)
         rest_out_q(banks_q1, 1)
@@ -394,8 +395,8 @@ def tile_iwht3layer_pa_s_kernel(tc, trans, weight, bias, grad_out, out):
         step_p0_one(0, 1)
         step_p0_one(1, 0)
         step_p0_one(1, 1)
+        step_q0(1, both[0:1], slice(1, SIDE))
         quantise_x(0, 1)
-        step_q0(1, both[0:1])
         step_p1(nc.gpsimd, 1, 0, low)
         rest_out_p(banks_first, 0)
         finish(0, 0)
@@ -404,10 +405,10 @@ def tile_iwht3layer_pa_s_kernel(tc, trans, weight, bias, grad_out, out):
         finish(0, 1)
         regroup(2, (3,))
         quantise_x(1, 1)
+        step_q0(1, both[1:2])
         finish(1, 0)
         keep_clock(1, 0, PASS_BANKS[6:8])
         regroup(3, (0, 1))
-        step_q0(1, both[1:2])
         step_p1(nc.gpsimd, 1, 0, high)
         rest_out_p(banks_last, 1)
         finish(1, 1)

@@ -37,8 +37,8 @@ PIXELS = SIDE * PACK * SIDE
 PLUS = ((0, 1, 2, 3), (0, 2), (0, 1), (0, 3))
 PAIRS = 8
 PAIR_COLS = 2 * K
-FIRST_BANKS = (1, 4, 5, 0)
-LAST_BANKS = (2, 3, 6, 7)
+FIRST_BANKS = (1, 4, 5, 2)
+LAST_BANKS = (3, 6, 7, 0)
 PASS_BANKS = FIRST_BANKS + FIRST_BANKS + LAST_BANKS + FIRST_BANKS
 
 
@@ -167,10 +167,12 @@ def tile_iwht3layer_pa_s_kernel(tc, trans, weight, bias, grad_out, out):
 
         def half_out_p(banks, v1):
             nc.scalar.activation(out=half_sums[v1][:], in_=by_channel(banks[0]), func=COPY, scale=0.5)
+
+        def half_round(v1):
             nc.scalar.copy(out=gy_by_place[:, 0, 0, 2 * v1 : 2 * v1 + 2, 0:K_PE, :], in_=half_sums[v1][:])
 
         def rest_out_p(banks, v1):
-            for u in (2, 1, 3):
+            for u in (1, 2, 3):
                 nc.vector.tensor_tensor(
                     out=gy_by_place[:, u % 2, u // 2, 2 * v1 : 2 * v1 + 2, 0:K_PE, :],
                     in0=by_channel(banks[u]),
@@ -363,39 +365,40 @@ def tile_iwht3layer_pa_s_kernel(tc, trans, weight, bias, grad_out, out):
         high = slice(1, 2)
         step_q0(0, both[0:1], slice(2, SIDE))
         step_q0(0, both[1:2], slice(2, 3))
-        step_p1(nc.vector, 0, 0, low)
+        step_q0(1, both[0:1], slice(0, 2))
         step_q0(0, both[1:2], slice(3, SIDE))
-        step_p1(nc.vector, 0, 1, low)
+        step_p1(nc.vector, 0, 0, low)
         step_p1(nc.gpsimd, 0, 0, high)
         step_p1(nc.gpsimd, 0, 1, high)
-        step_q0(1, both[0:1], slice(0, 1), nc.gpsimd)
+        step_p1(nc.gpsimd, 0, 1, low)
         rest_out_q(banks_q0, 0)
         half_out_q(banks_q1, 1)
         rest_out_q(banks_q1, 1)
         flipped = mm_turn(0)
-        banks_first = new_banks(FIRST_BANKS[0:3])
+        banks_first = new_banks(FIRST_BANKS)
         turn_p(banks_first, 0, 0)
         regroup(0, (1, 2, 3))
         mm_turn_out(flipped)
         sums = mm_transform(0)
         turn_p(banks_first, 0, 1)
         turn_p(banks_first, 0, 2)
-        regroup(1, (0,))
-        mm_out(sums)
-        banks_first.extend(new_banks(FIRST_BANKS[3:4]))
         turn_p(banks_first, 0, 3)
+        regroup(1, (0,))
         half_out_p(banks_first, 0)
+        mm_out(sums)
+        half_round(0)
         banks_last = new_banks(LAST_BANKS)
         for g in range(SIDE):
             turn_p(banks_last, 1, g)
         regroup(1, (1, 2, 3))
         regroup(2, (0, 1))
         half_out_p(banks_last, 1)
-        step_p0_one(0, 0)
-        step_p0_one(0, 1)
+        half_round(1)
         step_p0_one(1, 0)
         step_p0_one(1, 1)
-        step_q0(1, both[0:1], slice(1, SIDE))
+        step_p0_one(0, 0)
+        step_p0_one(0, 1)
+        step_q0(1, both[0:1], slice(2, SIDE))
         quantise_x(0, 1)
         step_p1(nc.gpsimd, 1, 0, low)
         rest_out_p(banks_first, 0)

from contextlib import ExitStack

import concourse.mybir as mybir
from concourse.masks import make_identity

FLOPS = 2 * 16 * 512 * 128 * 128
BYTES = 2 * (16 * 512 * 128) + 2 * (8 * 32 * 32 * 128) + 4 * (16 * 128 * 128)

BF16 = mybir.dt.bfloat16
F32 = mybir.dt.float32
U32 = mybir.dt.uint32
U8 = mybir.dt.uint8
I32 = mybir.dt.int32
E4M3_X4 = mybir.dt.float8_e4m3fn_x4
E5M2_X4 = mybir.dt.float8_e5m2_x4
ADD = mybir.AluOpType.add
SUB = mybir.AluOpType.subtract
COPY = mybir.ActivationFunctionType.Copy

PARTS = 128
PACK = 4
SIDE = 4
C = 128
K = 128
RUN = 4
N_PASS = 512
PAD_BLOCKS = N_PASS // K - 1
SLOTS = 2
PART_W = PACK // SLOTS
K_PE = PARTS // PART_W
K_MM = 12
MM_STEPS = K_MM // 2
K_VE = K - K_PE - K_MM
K_TOP = K_PE + K_VE
K_ROW = 56
PIXELS = SIDE * PACK * SIDE
PLUS = ((0, 1, 2, 3), (0, 2), (0, 1), (0, 3))
PAIRS = 8
PAIR_COLS = 2 * K
FIRST_BANKS = (1, 4, 5, 2)
LAST_BANKS = (3, 6, 7, 0)
PASS_BANKS = FIRST_BANKS + FIRST_BANKS + LAST_BANKS + FIRST_BANKS


def tile_iwht3layer_pa_s_kernel(tc, trans, weight, bias, grad_out, out):
    nc = tc.nc

    g_view = grad_out.rearrange(
        "b (i p) (h w q) k -> h p (b i) (w q k)", p=SIDE, h=2, w=PACK, q=SIDE
    )
    x_view = trans.rearrange("(u v) b i (h w) c -> (b i h) v u (w c)", v=SIDE, w=PACK)
    out_view = out.rearrange("(a b v) c k -> c v b a k", a=2, b=2)

    with ExitStack() as ctx:
        ctx.enter_context(tc.manual_schedule())
        keep = ctx.enter_context(tc.tile_pool(name="keep", bufs=1))
        outs = ctx.enter_context(tc.tile_pool(name="outs", bufs=4))
        psum = ctx.enter_context(tc.psum_pool(name="psum", bufs=1))

        def bank(i, shape, dtype):
            return psum.tile(shape, dtype, name="bank%d" % i, tag="bank%d" % i)

        ident_bf = keep.tile([PARTS, PARTS], BF16, name="ident_bf")
        make_identity(nc, ident_bf[:])
        ident = keep.tile([PARTS, PARTS], F32, name="ident")
        make_identity(nc, ident[:])

        g_raw = keep.tile([PARTS, SIDE, PACK * SIDE * K], BF16, name="g_raw")
        part_cols = PART_W * SIDE * K
        for s in range(SLOTS):
            for h in range(2):
                cols = slice(part_cols * s, part_cols * (s + 1))
                nc.sync.dma_start(out=g_raw[h:PARTS:2, 0, cols], in_=g_view[h, 0][:, cols])
        for p in range(1, SIDE):
            for h in range(2):
                nc.sync.dma_start(out=g_raw[h:PARTS:2, p, :], in_=g_view[h, p])
        g_views = [g_raw[:, p].rearrange("p (w q k) -> p w q k", w=PACK, q=SIDE) for p in range(SIDE)]
        x_raw = keep.tile([PARTS, SIDE * SIDE, PACK * C], BF16, name="x_raw")
        for v in range(SIDE):
            nc.sync.dma_start(out=x_raw[:, SIDE * v : SIDE * (v + 1), :], in_=x_view[:, v])

        warm = keep.tile([PARTS, 2], F32, name="warm")
        nc.vector.memset(warm[:, 0:1], 0.0)
        nc.scalar.activation(out=warm[:, 1:2], in_=warm[:, 0:1], func=COPY, scale=1.0)

        gy_width = (1 + PAIRS) * PAIR_COLS
        gy_codes = keep.tile([PARTS, gy_width], U32, name="gy_codes", align_bytes=64)
        gy_scales = keep.tile([PARTS, gy_width], U8, name="gy_scales", align_bytes=64)
        nc.vector.memset(gy_codes[:, 0:PAIR_COLS].bitcast(I32), 0)
        nc.vector.memset(gy_scales[:, 0:PAIR_COLS].bitcast(I32), 0)

        gy_grouped = keep.tile([PARTS, PAIRS, 2, K, PACK], BF16, name="gy_grouped", align_bytes=64)
        gy_by_place = gy_grouped[:].rearrange("p (v b) a k w -> p b a v k w", b=2)
        both = ((0, ADD), (1, SUB))

        def butterfly(dst, src):
            for bit, op in both:
                nc.vector.tensor_tensor(out=dst[:, bit], in0=src[:, 0], in1=src[:, 1], op=op)

        signs = [keep.tile([PARTS, PARTS], BF16, name="signs%d" % i) for i in range(4)]
        from_rows = ident_bf[:].rearrange("p (a b w q x) -> p b a q x w", a=2, b=2, w=PACK, q=SIDE)
        to_columns = signs[0][:].rearrange("p (q b a x w) -> p b a q x w", q=SIDE, b=2, a=2, x=2)
        for p0 in range(2):
            butterfly(to_columns[:, p0], from_rows[:, p0])
        butterfly(
            signs[1][:].rearrange("p (q b r) -> p b q r", q=SIDE, b=2),
            signs[0][:].rearrange("p (q b r) -> p b q r", q=SIDE, b=2),
        )
        butterfly(
            signs[2][:].rearrange("p (c r) -> p c r", c=2), signs[1][:].rearrange("p (c r) -> p c r", c=2)
        )
        butterfly(
            signs[3][:].rearrange("p (c d r) -> p d c r", c=2, d=2),
            signs[2][:].rearrange("p (c d r) -> p d c r", c=2, d=2),
        )
        hadamard = signs[3]

        g_f32 = [
            [keep.tile([PARTS, SIDE, PART_W, K_PE], F32, name="g_f32_%d_%d" % (s, p)) for p in range(SIDE)]
            for s in range(SLOTS)
        ]
        turned = [
            [keep.tile([PARTS, SIDE, PARTS], F32, name="turned%d_%d" % (s, v)) for v in range(SIDE)]
            for s in range(SLOTS)
        ]
        half_sums = [keep.tile([PARTS, 2, K_PE, PACK], F32, name="half_sum%d" % c) for c in range(2)]

        def cast(s, p):
            nc.scalar.activation(
                out=g_f32[s][p][:],
                in_=g_views[p][:, PART_W * s : PART_W * (s + 1), :, 0:K_PE].rearrange("p w q k -> p q w k"),
                func=COPY,
                scale=4.0,
            )

        def add_up(dst, terms):
            for i, term in enumerate(terms):
                nc.tensor.matmul(
                    out=dst,
                    lhsT=term,
                    rhs=ident[:],
                    is_transpose=True,
                    start=(i == 0),
                    stop=(i == len(terms) - 1),
                )

        def new_banks(places):
            return [bank(i, [PARTS, SIDE, PARTS], F32) for i in places]

        def turn_q(banks, s, p, g):
            add_up(banks[g][:, p, :], [g_f32[s][p][:, q].rearrange("p w k -> p (w k)") for q in PLUS[g]])

        def half_out_q(banks, s):
            nc.scalar.activation(out=turned[s][0][:], in_=banks[0][:], func=COPY, scale=0.5)

        def rest_out_q(banks, s):
            for v in range(1, SIDE):
                nc.vector.tensor_tensor(out=turned[s][v][:], in0=banks[v][:], in1=turned[s][0][:], op=SUB)

        def turn_p(banks, v1, g):
            for v0 in range(2):
                for s in range(SLOTS):
                    add_up(banks[g][:, SLOTS * v0 + s, :], [turned[s][2 * v1 + v0][:, p, :] for p in PLUS[g]])

        def by_channel(one_bank):
            return one_bank[:].rearrange("p r c -> p (r c)").rearrange("p (d w k) -> p d k w", d=2, w=PACK)

        def half_out_p(banks, v1):
            nc.scalar.activation(out=half_sums[v1][:], in_=by_channel(banks[0]), func=COPY, scale=0.5)

        def half_round(v1):
            nc.scalar.copy(out=gy_by_place[:, 0, 0, 2 * v1 : 2 * v1 + 2, 0:K_PE, :], in_=half_sums[v1][:])

        def rest_out_p(banks, v1):
            for u in (1, 2, 3):
                nc.vector.tensor_tensor(
                    out=gy_by_place[:, u % 2, u // 2, 2 * v1 : 2 * v1 + 2, 0:K_PE, :],
                    in0=by_channel(banks[u]),
                    in1=half_sums[v1][:],
                    op=SUB,
                )

        mm_raw = keep.tile([PARTS, MM_STEPS, PIXELS, 2], BF16, name="mm_raw")
        mm_turned = keep.tile([PARTS, MM_STEPS, PARTS], BF16, name="mm_turned")

        def mm_collect():
            nc.scalar.copy(
                out=mm_raw[:],
                in_=g_raw[:]
                .rearrange("p s (j k) -> p (s j) k", k=K)[:, :, K_TOP:K]
                .rearrange("p j (m x) -> p m j x", x=2),
            )

        def mm_turn(place):
            flipped = bank(place, [PARTS, 2 * SIDE, PARTS], BF16)
            for m in range(MM_STEPS):
                nc.tensor.transpose(
                    out=flipped[:, m, :], in_=mm_raw[:, m].rearrange("p j x -> p (j x)"), identity=ident_bf[:]
                )
            return flipped

        def mm_turn_out(flipped):
            nc.scalar.copy(out=mm_turned[:], in_=flipped[:, 0:MM_STEPS, :])

        def mm_transform(place):
            sums = bank(place, [PARTS, 2 * SIDE, PARTS], BF16)
            for m in range(MM_STEPS):
                nc.tensor.matmul(out=sums[:, m, :], lhsT=mm_turned[:, m, :], rhs=hadamard[:], start=True, stop=True)
            return sums

        def mm_out(sums):
            first = PACK * K_TOP
            nc.scalar.copy(
                out=gy_grouped[:]
                .rearrange("p n a k w -> p (n a) (k w)")[:, :, first : first + 2 * PACK * MM_STEPS]
                .rearrange("p j (m y) -> p j m y", y=2 * PACK),
                in_=sums[:, 0:MM_STEPS, :].rearrange("p m (j y) -> p j m y", y=2 * PACK),
            )

        half_q = [keep.tile([PARTS, SIDE, PACK, 2, K_VE], F32, name="half_q%d" % a) for a in range(2)]
        done_q = [keep.tile([PARTS, 2, SIDE, PACK, K_VE], F32, name="done_q%d" % a) for a in range(2)]
        half_p = [keep.tile([PARTS, 2, 2, PACK, 2, K_ROW], F32, name="half_p%d" % a) for a in range(2)]

        def step_q1(p, some=slice(0, PACK)):
            for v1, op in both:
                nc.vector.tensor_tensor(
                    out=half_q[v1][:, p, some],
                    in0=g_views[p][:, some, 0:2, K_PE:K_TOP],
                    in1=g_views[p][:, some, 2:4, K_PE:K_TOP],
                    op=op,
                )

        def step_q0(v1, some=both, rows=slice(0, SIDE), engine=nc.vector):
            for v0, op in some:
                engine.tensor_tensor(
                    out=done_q[v1][:, v0, rows],
                    in0=half_q[v1][:, rows, :, 0, :],
                    in1=half_q[v1][:, rows, :, 1, :],
                    op=op,
                )

        def step_p1(engine, v1, u1, some):
            src = done_q[v1][:].rearrange("p v (a b) w k -> p a v (b w) k", a=2)
            dst = half_p[v1][:].rearrange("p v b w a k -> p a v (b w) k")
            engine.tensor_tensor(
                out=dst[:, u1, some, :, 0:K_VE], in0=src[:, 0, some], in1=src[:, 1, some], op=both[u1][1]
            )

        def step_p0_one(v, u0, on_gpsimd=False):
            src = half_p[v // 2][:, v % 2, :, :, :, 0:K_VE]
            dst = gy_grouped[:, 2 * v + u0, :, K_PE:K_TOP, :]
            if not on_gpsimd:
                for u1 in range(2):
                    nc.vector.tensor_tensor(
                        out=dst[:, u1].rearrange("p (r e) w -> p r w e", e=RUN),
                        in0=src[:, 0, :, u1, :].rearrange("p w (r e) -> p r w e", e=RUN),
                        in1=src[:, 1, :, u1, :].rearrange("p w (r e) -> p r w e", e=RUN),
                        op=both[u0][1],
                    )
            else:
                nc.gpsimd.tensor_tensor(
                    out=dst,
                    in0=src[:, 0].rearrange("p w a k -> p a k w"),
                    in1=src[:, 1].rearrange("p w a k -> p a k w"),
                    op=both[u0][1],
                )

        x_grouped = keep.tile([PARTS, SIDE * SIDE, C, PACK], BF16, name="x_grouped", align_bytes=64)
        x_codes = keep.tile([PARTS, SIDE * SIDE, C], U32, name="x_codes", align_bytes=64)
        x_scales = keep.tile([PARTS, SIDE * SIDE, C], U8, name="x_scales", align_bytes=64)

        def regroup(v, some=(0, 1, 2, 3)):
            for u in some:
                t = SIDE * v + u
                nc.scalar.copy(
                    out=x_grouped[:, t].rearrange("p (r e) w -> p r w e", e=RUN),
                    in_=x_raw[:, t].rearrange("p (w r e) -> p r w e", w=PACK, e=RUN),
                )

        def quantise_x(v, count):
            start = SIDE * v
            stop = SIDE * (v + count)
            nc.vector.quantize_mx(
                out=x_codes[:, start:stop].rearrange("p t c -> p (t c)").bitcast(E4M3_X4),
                scales=x_scales[:, start:stop].rearrange("p t c -> p (t c)"),
                in_=x_grouped[:, start:stop].rearrange("p t c w -> p (t c w)"),
            )

        def finish(v, u0, one_by_one=False):
            pair = 2 * v + u0
            first = (1 + pair) * PAIR_COLS
            if not one_by_one:
                nc.vector.quantize_mx(
                    out=gy_codes[:, first : first + PAIR_COLS].bitcast(E5M2_X4),
                    scales=gy_scales[:, first : first + PAIR_COLS],
                    in_=gy_grouped[:, pair].rearrange("p a k w -> p (a k w)"),
                )
            result = outs.tile([PARTS, 2, K], F32, name="result", tag="result")
            for u1 in range(2):
                if one_by_one:
                    nc.vector.quantize_mx(
                        out=gy_codes[:, first + K * u1 : first + K * (u1 + 1)].bitcast(E5M2_X4),
                        scales=gy_scales[:, first + K * u1 : first + K * (u1 + 1)],
                        in_=gy_grouped[:, pair, u1].rearrange("p k w -> p (k w)"),
                    )
                stop = first + (K * (u1 + 1) if one_by_one else PAIR_COLS)
                wanted = N_PASS - (stop - first) + K * u1
                acc = bank(PASS_BANKS[2 * pair + u1], [PARTS, N_PASS], F32)
                t = SIDE * v + 2 * u1 + u0
                nc.tensor.matmul_mx(
                    out=acc[:],
                    lhsT=x_codes[:, t, :].bitcast(E4M3_X4),
                    lhsT_scale=x_scales[:, t, :],
                    rhs=gy_codes[:, stop - N_PASS : stop].bitcast(E5M2_X4),
                    rhs_scale=gy_scales[:, stop - N_PASS : stop],
                    start=True,
                    stop=True,
                )
                nc.scalar.activation(
                    out=result[:, u1, :], in_=acc[:, wanted : wanted + K], func=COPY, scale=1.0 / (SIDE * SIDE)
                )
                if one_by_one:
                    nc.sync.dma_start(out=out_view[:, v, u0, u1], in_=result[:, u1, :])
            if not one_by_one:
                nc.sync.dma_start(out=out_view[:, v, u0], in_=result[:])

        def keep_clock(v, u0, places):
            stop = (2 + 2 * v + u0) * PAIR_COLS
            for u1, place in enumerate(places):
                spare = bank(place, [PARTS, N_PASS], F32)
                t = SIDE * v + 2 * u1 + u0
                nc.tensor.matmul_mx(
                    out=spare[:],
                    lhsT=x_codes[:, t, :].bitcast(E4M3_X4),
                    lhsT_scale=x_scales[:, t, :],
                    rhs=gy_codes[:, stop - N_PASS : stop].bitcast(E5M2_X4),
                    rhs_scale=gy_scales[:, stop - N_PASS : stop],
                    start=True,
                    stop=True,
                )

        banks_q0 = new_banks((0, 1, 2, 3))
        for p in range(SIDE):
            cast(0, p)
            if p < 3:
                cast(1, p)
            if p == 0:
                step_q1(p, slice(0, PART_W))
                step_q1(p, slice(PART_W, PACK))
            else:
                step_q1(p)
            if p < 2:
                step_q0(0, both, slice(p, p + 1))
            for g in range(SIDE):
                turn_q(banks_q0, 0, p, g)
        cast(1, 3)
        regroup(0, (0,))
        half_out_q(banks_q0, 0)
        mm_collect()
        banks_q1 = new_banks((4, 5, 6, 7))
        for g in range(SIDE):
            for p in range(SIDE):
                turn_q(banks_q1, 1, p, g)
        low = slice(0, 1)
        high = slice(1, 2)
        step_q0(0, both[0:1], slice(2, SIDE))
        step_q0(0, both[1:2], slice(2, 3))
        step_q0(1, both[0:1], slice(0, 2))
        step_q0(0, both[1:2], slice(3, SIDE))
        step_p1(nc.vector, 0, 0, low)
        step_p1(nc.gpsimd, 0, 0, high)
        step_p1(nc.gpsimd, 0, 1, high)
        step_p1(nc.gpsimd, 0, 1, low)
        rest_out_q(banks_q0, 0)
        half_out_q(banks_q1, 1)
        rest_out_q(banks_q1, 1)
        flipped = mm_turn(0)
        banks_first = new_banks(FIRST_BANKS)
        turn_p(banks_first, 0, 0)
        regroup(0, (1, 2, 3))
        mm_turn_out(flipped)
        sums = mm_transform(0)
        turn_p(banks_first, 0, 1)
        turn_p(banks_first, 0, 2)
        turn_p(banks_first, 0, 3)
        regroup(1, (0,))
        half_out_p(banks_first, 0)
        mm_out(sums)
        half_round(0)
        banks_last = new_banks(LAST_BANKS)
        for g in range(SIDE):
            turn_p(banks_last, 1, g)
        regroup(1, (1, 2, 3))
        regroup(2, (0, 1))
        half_out_p(banks_last, 1)
        half_round(1)
        step_p0_one(1, 0)
        step_p0_one(1, 1)
        step_p0_one(0, 0)
        step_p0_one(0, 1)
        step_q0(1, both[0:1], slice(2, SIDE))
        quantise_x(0, 1)
        step_p1(nc.gpsimd, 1, 0, low)
        rest_out_p(banks_first, 0)
        finish(0, 0)
        regroup(2, (2,))
        step_p1(nc.vector, 1, 1, low)
        finish(0, 1)
        regroup(2, (3,))
        quantise_x(1, 1)
        step_q0(1, both[1:2])
        finish(1, 0)
        keep_clock(1, 0, PASS_BANKS[6:8])
        regroup(3, (0, 1))
        step_p1(nc.gpsimd, 1, 0, high)
        rest_out_p(banks_last, 1)
        finish(1, 1)
        keep_clock(1, 1, PASS_BANKS[8:10])
        regroup(3, (2, 3))
        step_p1(nc.vector, 1, 1, high)
        step_p0_one(2, 0)
        step_p0_one(2, 1)
        quantise_x(2, 1)
        finish(2, 0)
        step_p0_one(3, 0)
        finish(2, 1)
        quantise_x(3, 1)
        finish(3, 0)
        step_p0_one(3, 1)
        finish(3, 1, True)
